import numpy as np
import ml_dtypes


def mxq(x, axis, fmt="e4m3"):
    dtype, down = {"e4m3": (ml_dtypes.float8_e4m3fn, 7), "e5m2": (ml_dtypes.float8_e5m2, 14)}[fmt]
    v = np.moveaxis(np.asarray(x, np.float32).astype(ml_dtypes.bfloat16).astype(np.float64), axis, -1)
    blocks = v.reshape(v.shape[:-1] + (-1, 32))
    amax = np.abs(blocks).max(-1, keepdims=True)
    byte = np.maximum(np.where(amax > 0, np.frexp(amax)[1] - 1 + 127, 0) - down, 1)
    scale = np.exp2(byte - 127.0)
    codes = (blocks / scale).astype(np.float32).astype(dtype).astype(np.float64)
    return np.moveaxis((codes * scale).reshape(v.shape), -1, axis)


WIDE = False


def mx_kscale(k):
    if not WIDE:
        return np.ones(k)
    levels = np.array([10, -10, 5, -5, 0])
    if k % 512:
        return np.exp2(np.random.permutation(np.resize(levels, k // 32))).repeat(32)
    a = np.empty((k // 512, 16))
    for p in range(k // 512):
        a[p, :8] = np.random.permutation(np.resize(levels, 8))
        for g in range(8):
            far = levels[np.abs(levels - a[p, g]) >= 10]
            a[p, g + 8] = far[np.random.randint(len(far))]
    return np.exp2(a.ravel()).repeat(32)


BF16 = ml_dtypes.bfloat16


def bf(x):
    return np.asarray(x, np.float32).astype(BF16)


def f64(x):
    return np.asarray(x).astype(np.float64)


B, T, DX, DY, F = 128, 8, 1024, 1024, 5
MIN_CONTEXT = 1
G = 1.5 / DY ** 0.25


def setup_inputs():
    s, t = mx_kscale(DX), mx_kscale(DY)
    return {"embeddings": bf(np.random.standard_normal((B, T, DX)) * s),
            "contexts": bf(np.random.standard_normal((B, T, DY)) * G / t),
            "W": bf(np.random.standard_normal((F, DY, DX)) * G / np.sqrt(DX) * t[:, None] / s)}


def reference(embeddings, contexts, W):
    eq = mxq(f64(embeddings)[:, MIN_CONTEXT:T], 2, "e4m3")
    cq = mxq(f64(contexts)[:, MIN_CONTEXT - 1:T - 1], 2, "e4m3")
    wq = mxq(f64(W), 2, "e4m3")
    losses = []
    for step in range(F):
        S = T - step - MIN_CONTEXT
        xw = eq[:, step:] @ wq[step].T
        scores = mxq(xw, 2, "e4m3").transpose(1, 0, 2) @ cq[:, :S].transpose(1, 2, 0)
        pos = np.diagonal(scores, axis1=1, axis2=2)
        m = scores.max(2, keepdims=True)
        lse = np.log(np.exp(scores - m).sum(2)) + m[:, :, 0] - np.log(B * S)
        losses.append((lse - pos).T.reshape(-1))
    return np.concatenate(losses)

@@ -1,0 +1,343 @@
+from contextlib import ExitStack
+
+import concourse.mybir as mybir
+from concourse.masks import make_identity
+
+F32 = mybir.dt.float32
+BF16 = mybir.dt.bfloat16
+U32 = mybir.dt.uint32
+U8 = mybir.dt.uint8
+FP8X4 = mybir.dt.float8_e4m3fn_x4
+ALU = mybir.AluOpType
+ACT = mybir.ActivationFunctionType
+AX = mybir.AxisListType
+
+P = 128
+FEAT = 1024
+N_STEP = 5
+N_SLICE = 7
+TILE_WORDS = FEAT // 4
+GROUP0 = [0, 7, 13, 18, 22]
+N_GROUP = 25
+B_LO = 8
+B_HI = P // B_LO
+W_BUFFERS = 7
+FLOPS = 2 * N_GROUP * P * FEAT * FEAT + 2 * N_GROUP * P * P * FEAT
+
+
+def tile_infonceloss_pa_kernel(tc, embeddings, contexts, W, out):
+    nc = tc.nc
+    with ExitStack() as ctx:
+        const = ctx.enter_context(tc.tile_pool(name="const", bufs=1))
+        raw = ctx.enter_context(tc.tile_pool(name="raw", bufs=1))
+        wraw_pool = ctx.enter_context(tc.tile_pool(name="wraw", bufs=W_BUFFERS))
+        grp_pool = ctx.enter_context(tc.tile_pool(name="grp", bufs=4))
+        keep = ctx.enter_context(tc.tile_pool(name="keep", bufs=1))
+        xwg_pool = ctx.enter_context(tc.tile_pool(name="xwg", bufs=4))
+        junk = ctx.enter_context(tc.tile_pool(name="junk", bufs=2))
+        ring = ctx.enter_context(tc.psum_pool(name="ring", bufs=6))
+        scp = ctx.enter_context(tc.psum_pool(name="scores", bufs=2))
+        ctx.enter_context(tc.manual_schedule())
+
+        x_raw = raw.tile([P, N_SLICE, FEAT], BF16, name="x_raw")
+        c_raw = raw.tile([P, N_SLICE, FEAT], BF16, name="c_raw")
+        w_raw = {}
+
+        def load_x(t0, t1):
+            nc.sync.dma_start(out=x_raw[:, t0:t1, :], in_=embeddings[:, 1 + t0 : 1 + t1, :])
+
+        def load_c(t0, t1):
+            nc.sync.dma_start(out=c_raw[:, t0:t1, :], in_=contexts[:, t0:t1, :])
+
+        def load_w(half, pieces=1):
+            k, g = half // 2, half % 2
+            w_half = wraw_pool.tile([P, 4, FEAT], BF16, name="w_raw", tag="w_raw")
+            src = W[k, 512 * g : 512 * (g + 1), :].rearrange("(p t) d -> p t d", t=4)
+            step = 4 // pieces
+            for t in range(0, 4, step):
+                nc.sync.dma_start(out=w_half[:, t : t + step, :], in_=src[:, t : t + step, :])
+            w_raw[half] = w_half
+
+        load_x(0, 1)
+        load_w(0, pieces=2)
+        load_x(1, 2)
+        load_x(2, 4)
+        load_x(4, 7)
+        load_w(1)
+        load_w(2)
+        load_w(3)
+        load_c(0, 4)
+        load_c(4, 7)
+        load_w(4)
+        load_w(5)
+        load_w(6)
+
+        ident = const.tile([P, P], F32, name="ident")
+        make_identity(nc, ident[:])
+        warm = const.tile([P, 2], F32, name="warm")
+        nc.vector.memset(warm[:], 1.0)
+        nc.scalar.activation(out=warm[:, 1:2], in_=warm[:, 0:1], func=ACT.Exp)
+        mask8 = const.tile([P, B_LO], F32, name="mask8")
+        nc.vector.tensor_reduce(
+            out=mask8[:], in_=ident[:].rearrange("p (q l) -> p l q", l=B_LO), axis=AX.X, op=ALU.add
+        )
+        fold = const.tile([P, P], F32, name="fold")
+        nc.vector.memset(fold[:], 0.0)
+        nc.vector.tensor_reduce(
+            out=fold[:, 0:B_HI], in_=ident[:].rearrange("p (q l) -> p q l", l=B_LO), axis=AX.X, op=ALU.add
+        )
+
+        xq = keep.tile([P, N_SLICE, TILE_WORDS], U32, name="xq", align_bytes=64)
+        xs = keep.tile([P, N_SLICE, TILE_WORDS], U8, name="xs", align_bytes=64)
+        cq = keep.tile([P, N_SLICE, TILE_WORDS], U32, name="cq", align_bytes=64)
+        cs = keep.tile([P, N_SLICE, TILE_WORDS], U8, name="cs", align_bytes=64)
+        wq = [keep.tile([P, 8, TILE_WORDS], U32, name="wq%d" % k, align_bytes=64) for k in range(N_STEP)]
+        ws = [keep.tile([P, 8, TILE_WORDS], U8, name="ws%d" % k, align_bytes=64) for k in range(N_STEP)]
+        xwq = keep.tile([P, 2 * N_GROUP, P], U32, name="xwq", align_bytes=64)
+        xws = keep.tile([P, 2 * N_GROUP, P], U8, name="xws", align_bytes=64)
+        negmax = keep.tile([P, N_GROUP], F32, name="negmax")
+        sumexp = keep.tile([P, N_GROUP], F32, name="sumexp")
+        dm = keep.tile([P, N_GROUP], F32, name="dm")
+        spread_s = keep.tile([P, B_LO * N_GROUP], F32, name="spread_s")
+        spread_d = keep.tile([P, B_LO * N_GROUP], F32, name="spread_d")
+
+        def flat(ap):
+            return ap.rearrange("p i c -> p (i c)")
+
+        def quantise(codes, scales, values):
+            nc.vector.quantize_mx(out=flat(codes).bitcast(FP8X4), scales=flat(scales), in_=flat(values))
+
+        def quantise_tiles(grp, n, codes, scales, widest):
+            i0 = 0
+            for w in (4, 2, 1):
+                if w <= widest:
+                    for call in range((n - i0) // w):
+                        quantise(codes[:, i0 : i0 + w, :], scales[:, i0 : i0 + w, :], grp[:, i0 : i0 + w, :])
+                        i0 += w
+
+        def transposes(rows):
+            grp = grp_pool.tile([P, 4, FEAT], BF16, name="grp", tag="grp", align_bytes=64)
+            for i in range(len(rows)):
+                bank = ring.tile([P, 4, P], F32, name="bank", tag="bank")
+                words = rows[i].bitcast(F32)
+                for j in range(4):
+                    first = 256 * (j // 2) + j % 2
+                    nc.tensor.transpose(bank[:, j, :], words[:, first : 256 * (j // 2 + 1) : 2], ident[:])
+                dst = grp[:, i, :].bitcast(F32).rearrange("p (g r u) -> p g r u", g=2, u=2)
+                src = bank[:].rearrange("p (g u) r -> p g r u", u=2)
+                if i % 2 == 0:
+                    nc.vector.tensor_copy(out=dst, in_=src)
+                else:
+                    nc.scalar.copy(out=dst, in_=src)
+            return grp
+
+        def operand(kind, a, b):
+            if kind == "x":
+                return [x_raw[:, t, :] for t in range(a, b)], xq[:, a:b, :], xs[:, a:b, :]
+            if kind == "c":
+                return [c_raw[:, t, :] for t in range(a, b)], cq[:, a:b, :], cs[:, a:b, :]
+            k, g = a // 2, a % 2
+            tiles = slice(4 * g, 4 * g + 4)
+            return [w_raw[a][:, j, :] for j in range(4)], wq[k][:, tiles, :], ws[k][:, tiles, :]
+
+        def xw_row(k, g2, s):
+            return 2 * GROUP0[k] + g2 * (N_SLICE - k) + s
+
+        def stage1(k, g2, slices):
+            xwg = xwg_pool.tile([P, 2, 512], BF16, name="xwg", tag="xwg", align_bytes=64)
+            for i in range(len(slices)):
+                s = slices[i]
+                bank = ring.tile([P, 4, P], F32, name="bank", tag="bank")
+                for t in range(4):
+                    for g1 in range(2):
+                        cols = slice(P * g1, P * (g1 + 1))
+                        nc.tensor.matmul_mx(
+                            out=bank[:, t, :],
+                            lhsT=wq[k][:, 4 * g2 + t, cols].bitcast(FP8X4),
+                            lhsT_scale=ws[k][:, 4 * g2 + t, cols],
+                            rhs=xq[:, k + s, cols].bitcast(FP8X4),
+                            rhs_scale=xs[:, k + s, cols],
+                            start=(g1 == 0),
+                            stop=(g1 == 1),
+                        )
+                nc.scalar.copy(
+                    out=xwg[:, i, :].rearrange("p (b t) -> p b t", t=4),
+                    in_=bank[:].rearrange("p t b -> p b t"),
+                )
+            return xwg
+
+        def quantise_xw(k, g2, slices, xwg):
+            n = len(slices)
+            r0 = xw_row(k, g2, slices[0])
+            quantise(xwq[:, r0 : r0 + n, :], xws[:, r0 : r0 + n, :], xwg[:, 0:n, :])
+
+        score_banks = {}
+
+        def scores(k, first_slices):
+            n_s = N_SLICE - k
+            score_banks[k] = []
+            for j in range(len(first_slices)):
+                s0 = first_slices[j]
+                n = (first_slices[j + 1] if j + 1 < len(first_slices) else n_s) - s0
+                sc = scp.tile([P, 4, P], F32, name="sc", tag="sc")
+                for i in range(n):
+                    for g2 in range(2):
+                        r = xw_row(k, g2, s0 + i)
+                        cols = slice(P * g2, P * (g2 + 1))
+                        nc.tensor.matmul_mx(
+                            out=sc[:, i, :],
+                            lhsT=xwq[:, r, :].bitcast(FP8X4),
+                            lhsT_scale=xws[:, r, :],
+                            rhs=cq[:, s0 + i, cols].bitcast(FP8X4),
+                            rhs_scale=cs[:, s0 + i, cols],
+                            start=(g2 == 0),
+                            stop=(g2 == 1),
+                        )
+                score_banks[k].append((sc, GROUP0[k] + s0, n))
+
+        def row_max(k, b):
+            sc, gi, n = score_banks[k][b]
+            nc.vector.tensor_reduce(out=negmax[:, gi : gi + n], in_=sc[:, 0:n, :], axis=AX.X, op=ALU.max, negate=True)
+
+        def diagonal(k, b):
+            sc, gi, n = score_banks[k][b]
+            for i in range(n):
+                jv = junk.tile([P, P], F32, name="jv", tag="jv")
+                nc.vector.scalar_tensor_tensor(
+                    out=jv[:],
+                    in0=sc[:, i, :],
+                    scalar=negmax[:, gi + i : gi + i + 1],
+                    in1=ident[:],
+                    op0=ALU.add,
+                    op1=ALU.mult,
+                    accum_out=dm[:, gi + i : gi + i + 1],
+                )
+
+        def exponentials(k, b):
+            sc, gi, n = score_banks[k][b]
+            for i in range(n):
+                js = junk.tile([P, P], F32, name="js", tag="js")
+                nc.scalar.activation(
+                    out=js[:],
+                    in_=sc[:, i, :],
+                    func=ACT.Exp,
+                    bias=negmax[:, gi + i : gi + i + 1],
+                    scale=1.0,
+                    accum_out=sumexp[:, gi + i : gi + i + 1],
+                )
+
+        def step_columns(tile, k):
+            g0 = GROUP0[k]
+            return tile[:, B_LO * g0 : B_LO * (g0 + N_SLICE - k)].rearrange("p (l s) -> p l s", l=B_LO)
+
+        def spread_diagonal(k):
+            n_s = N_SLICE - k
+            shape = [P, B_LO, n_s]
+            nc.vector.tensor_tensor(
+                out=step_columns(spread_d, k),
+                in0=dm[:, GROUP0[k] : GROUP0[k] + n_s].unsqueeze(1).to_broadcast(shape),
+                in1=mask8[:].unsqueeze(2).to_broadcast(shape),
+                op=ALU.mult,
+            )
+
+        def spread_sum(k):
+            n_s = N_SLICE - k
+            shape = [P, B_LO, n_s]
+            nc.vector.scalar_tensor_tensor(
+                out=step_columns(spread_s, k),
+                in0=sumexp[:, GROUP0[k] : GROUP0[k] + n_s].unsqueeze(1).to_broadcast(shape),
+                scalar=1.0 / (P * n_s),
+                in1=mask8[:].unsqueeze(2).to_broadcast(shape),
+                op0=ALU.mult,
+                op1=ALU.mult,
+            )
+
+        chunks = []
+        last_chunk = []
+        for k in range(N_STEP):
+            for g2 in range(2):
+                for s in range(0, N_SLICE - k, 2):
+                    chunks.append((k, g2, list(range(s, min(s + 2, N_SLICE - k)))))
+            last_chunk.append(len(chunks) - 1)
+        groups = [[("x", 0, 1), ("w", 0, 0), ("x", 1, 2), ("x", 2, 4)], [("x", 4, 7)], [("w", 1, 0)], [("w", 2, 0)]]
+        groups += [[("w", 3, 0)], [("c", 0, 4)], [("c", 4, 7)]] + [[("w", half, 0)] for half in range(4, 2 * N_STEP)]
+        contexts_ready = 12
+        scores_before = [max(last_chunk[k] + 3, contexts_ready) for k in range(N_STEP - 1)]
+        n_groups = 0
+        unquantised = None
+        step = -1
+        since = 0
+        for j in range(len(chunks)):
+            staged = []
+            if n_groups < len(groups) and (j < 2 or j % 2 == 0):
+                for kind, a, b in groups[n_groups]:
+                    rows, codes, scales = operand(kind, a, b)
+                    grp = transposes(rows)
+                    if j == 0:
+                        quantise_tiles(grp, len(rows), codes, scales, 2)
+                    else:
+                        staged.append((grp, len(rows), codes, scales))
+                    if kind == "w" and a + W_BUFFERS < 2 * N_STEP:
+                        load_w(a + W_BUFFERS)
+                n_groups += 1
+            if unquantised is not None:
+                quantise_xw(unquantised[0], unquantised[1], unquantised[2], unquantised[3])
+            for grp, n, codes, scales in staged:
+                quantise_tiles(grp, n, codes, scales, 4)
+            since += 1
+            if j in scores_before:
+                step += 1
+                since = 0
+                scores(step, (0, 4) if N_SLICE - step > 4 else (0,))
+            k, g2, slices = chunks[j]
+            unquantised = (k, g2, slices, stage1(k, g2, slices))
+            if step >= 0:
+                two_banks = len(score_banks[step]) > 1
+                if since == 0:
+                    row_max(step, 0)
+                    diagonal(step, 0)
+                if since == 1:
+                    exponentials(step, 0)
+                    if two_banks:
+                        row_max(step, 1)
+                        diagonal(step, 1)
+                if since == 2 and two_banks:
+                    exponentials(step, 1)
+                if since == 3:
+                    spread_diagonal(step)
+                    spread_sum(step)
+        quantise_xw(unquantised[0], unquantised[1], unquantised[2], unquantised[3])
+
+        last = N_STEP - 1
+        n_col = B_LO * N_GROUP
+        n_early = B_LO * GROUP0[last]
+        scores(last, (0, 2))
+        row_max(last, 0)
+        row_max(last, 1)
+        exponentials(last, 0)
+        exponentials(last, 1)
+        nc.scalar.activation(out=warm[:, 1:2], in_=sumexp[:, N_GROUP - 1 : N_GROUP], func=ACT.Ln)
+        spread_diagonal(last - 1)
+        spread_sum(last - 1)
+        zs = ring.tile([P, 512], F32, name="zs", tag="bank")
+        zd = ring.tile([P, 512], F32, name="zd", tag="bank")
+        nc.tensor.matmul(zs[:, 0:n_early], lhsT=fold[:], rhs=spread_s[:, 0:n_early], start=True, stop=True)
+        nc.tensor.matmul(zd[:, 0:n_early], lhsT=fold[:], rhs=spread_d[:, 0:n_early], start=True, stop=True)
+        spread_sum(last)
+        nc.tensor.matmul(zs[:, n_early:n_col], lhsT=fold[:], rhs=spread_s[:, n_early:n_col], start=True, stop=True)
+        diagonal(last, 0)
+        diagonal(last, 1)
+        spread_diagonal(last)
+        nc.tensor.matmul(zd[:, n_early:n_col], lhsT=fold[:], rhs=spread_d[:, n_early:n_col], start=True, stop=True)
+        lnz = keep.tile([P, n_col], F32, name="lnz")
+        nc.scalar.activation(out=lnz[0:B_HI, :], in_=zs[0:B_HI, 0:n_col], func=ACT.Ln)
+        res = keep.tile([P, n_col], F32, name="res")
+        nc.vector.tensor_tensor(out=res[0:B_HI, :], in0=lnz[0:B_HI, :], in1=zd[0:B_HI, 0:n_col], op=ALU.subtract)
+        for k in range(N_STEP):
+            n_s = N_SLICE - k
+            g0 = GROUP0[k]
+            queue = nc.sync if k % 2 == 0 else nc.scalar
+            queue.dma_start(
+                out=out[P * g0 : P * (g0 + n_s)].rearrange("(q c) -> q c", q=B_HI),
+                in_=res[0:B_HI, B_LO * g0 : B_LO * (g0 + n_s)],
+            )

@@ -21,7 +21,7 @@ GROUP0 = [0, 7, 13, 18, 22]
 N_GROUP = 25
 B_LO = 8
 B_HI = P // B_LO
-W_BUFFERS = 7
+W_BUFFERS = 5
 FLOPS = 2 * N_GROUP * P * FEAT * FEAT + 2 * N_GROUP * P * P * FEAT
 
 
@@ -31,6 +31,7 @@ def tile_infonceloss_pa_kernel(tc, embeddings, contexts, W, out):
         const = ctx.enter_context(tc.tile_pool(name="const", bufs=1))
         raw = ctx.enter_context(tc.tile_pool(name="raw", bufs=1))
         wraw_pool = ctx.enter_context(tc.tile_pool(name="wraw", bufs=W_BUFFERS))
+        split_pool = ctx.enter_context(tc.tile_pool(name="split", bufs=3))
         grp_pool = ctx.enter_context(tc.tile_pool(name="grp", bufs=4))
         keep = ctx.enter_context(tc.tile_pool(name="keep", bufs=1))
         xwg_pool = ctx.enter_context(tc.tile_pool(name="xwg", bufs=4))
@@ -69,8 +70,6 @@ def tile_infonceloss_pa_kernel(tc, embeddings, contexts, W, out):
         load_c(0, 4)
         load_c(4, 7)
         load_w(4)
-        load_w(5)
-        load_w(6)
 
         ident = const.tile([P, P], F32, name="ident")
         make_identity(nc, ident[:])
@@ -115,17 +114,29 @@ def tile_infonceloss_pa_kernel(tc, embeddings, contexts, W, out):
                         quantise(codes[:, i0 : i0 + w, :], scales[:, i0 : i0 + w, :], grp[:, i0 : i0 + w, :])
                         i0 += w
 
-        def transposes(rows):
+        def split_words(raw_tiles, n):
+            split = split_pool.tile([P, 4, FEAT], BF16, name="split", tag="split")
+            nc.vector.tensor_copy(
+                out=flat(split[:, 0:n, :]).bitcast(F32).rearrange("p (a u r) -> p a u r", u=2, r=P),
+                in_=flat(raw_tiles).bitcast(F32).rearrange("p (a r u) -> p a u r", u=2, r=P),
+            )
+            return [split[:, i, :] for i in range(n)]
+
+        def transposes(rows, is_split, on_vector):
             grp = grp_pool.tile([P, 4, FEAT], BF16, name="grp", tag="grp", align_bytes=64)
             for i in range(len(rows)):
                 bank = ring.tile([P, 4, P], F32, name="bank", tag="bank")
                 words = rows[i].bitcast(F32)
                 for j in range(4):
-                    first = 256 * (j // 2) + j % 2
-                    nc.tensor.transpose(bank[:, j, :], words[:, first : 256 * (j // 2 + 1) : 2], ident[:])
+                    g, u = j // 2, j % 2
+                    if is_split:
+                        col = words[:, P * j : P * (j + 1)]
+                    else:
+                        col = words[:, 256 * g + u : 256 * (g + 1) : 2]
+                    nc.tensor.transpose(bank[:, j, :], col, ident[:])
                 dst = grp[:, i, :].bitcast(F32).rearrange("p (g r u) -> p g r u", g=2, u=2)
                 src = bank[:].rearrange("p (g u) r -> p g r u", u=2)
-                if i % 2 == 0:
+                if i in on_vector:
                     nc.vector.tensor_copy(out=dst, in_=src)
                 else:
                     nc.scalar.copy(out=dst, in_=src)
@@ -133,12 +144,12 @@ def tile_infonceloss_pa_kernel(tc, embeddings, contexts, W, out):
 
         def operand(kind, a, b):
             if kind == "x":
-                return [x_raw[:, t, :] for t in range(a, b)], xq[:, a:b, :], xs[:, a:b, :]
+                return x_raw[:, a:b, :], b - a, xq[:, a:b, :], xs[:, a:b, :]
             if kind == "c":
-                return [c_raw[:, t, :] for t in range(a, b)], cq[:, a:b, :], cs[:, a:b, :]
+                return c_raw[:, a:b, :], b - a, cq[:, a:b, :], cs[:, a:b, :]
             k, g = a // 2, a % 2
             tiles = slice(4 * g, 4 * g + 4)
-            return [w_raw[a][:, j, :] for j in range(4)], wq[k][:, tiles, :], ws[k][:, tiles, :]
+            return w_raw[a][:], 4, wq[k][:, tiles, :], ws[k][:, tiles, :]
 
         def xw_row(k, g2, s):
             return 2 * GROUP0[k] + g2 * (N_SLICE - k) + s
@@ -264,6 +275,15 @@ def tile_infonceloss_pa_kernel(tc, embeddings, contexts, W, out):
         contexts_ready = 12
         scores_before = [max(last_chunk[k] + 3, contexts_ready) for k in range(N_STEP - 1)]
         n_groups = 0
+        split_rows = {}
+
+        def split_group(i):
+            for kind, a, b in groups[i]:
+                raw_tiles, n = operand(kind, a, b)[0:2]
+                split_rows[i] = split_words(raw_tiles, n)
+                if kind == "w" and a + W_BUFFERS < 2 * N_STEP:
+                    load_w(a + W_BUFFERS)
+
         unquantised = None
         step = -1
         since = 0
@@ -271,14 +291,15 @@ def tile_infonceloss_pa_kernel(tc, embeddings, contexts, W, out):
             staged = []
             if n_groups < len(groups) and (j < 2 or j % 2 == 0):
                 for kind, a, b in groups[n_groups]:
-                    rows, codes, scales = operand(kind, a, b)
-                    grp = transposes(rows)
+                    raw_tiles, n, codes, scales = operand(kind, a, b)
                     if j == 0:
-                        quantise_tiles(grp, len(rows), codes, scales, 2)
+                        grp = transposes([raw_tiles[:, i, :] for i in range(n)], False, (0, 2))
+                        quantise_tiles(grp, n, codes, scales, 2)
+                        if kind == "w":
+                            load_w(a + W_BUFFERS)
                     else:
-                        staged.append((grp, len(rows), codes, scales))
-                    if kind == "w" and a + W_BUFFERS < 2 * N_STEP:
-                        load_w(a + W_BUFFERS)
+                        grp = transposes(split_rows[n_groups], True, (3,) if kind == "w" else (1, 3))
+                        staged.append((grp, n, codes, scales))
                 n_groups += 1
             if unquantised is not None:
                 quantise_xw(unquantised[0], unquantised[1], unquantised[2], unquantised[3])
@@ -306,6 +327,11 @@ def tile_infonceloss_pa_kernel(tc, embeddings, contexts, W, out):
                 if since == 3:
                     spread_diagonal(step)
                     spread_sum(step)
+            if j < 2 or j % 2 == 0:
+                if j == 0:
+                    split_group(1)
+                if n_groups + 1 < len(groups):
+                    split_group(n_groups + 1)
         quantise_xw(unquantised[0], unquantised[1], unquantised[2], unquantised[3])
 
         last = N_STEP - 1

@@ -34,10 +34,10 @@ def tile_infonceloss_pa_kernel(tc, embeddings, contexts, W, out):
         split_pool = ctx.enter_context(tc.tile_pool(name="split", bufs=3))
         grp_pool = ctx.enter_context(tc.tile_pool(name="grp", bufs=4))
         keep = ctx.enter_context(tc.tile_pool(name="keep", bufs=1))
-        xwg_pool = ctx.enter_context(tc.tile_pool(name="xwg", bufs=4))
+        xwg_pool = ctx.enter_context(tc.tile_pool(name="xwg", bufs=2))
         junk = ctx.enter_context(tc.tile_pool(name="junk", bufs=2))
         ring = ctx.enter_context(tc.psum_pool(name="ring", bufs=6))
-        scp = ctx.enter_context(tc.psum_pool(name="scores", bufs=2))
+        scp = ctx.enter_context(tc.psum_pool(name="scores", bufs=8 - 6))
         ctx.enter_context(tc.manual_schedule())
 
         x_raw = raw.tile([P, N_SLICE, FEAT], BF16, name="x_raw")
@@ -59,17 +59,13 @@ def tile_infonceloss_pa_kernel(tc, embeddings, contexts, W, out):
                 nc.sync.dma_start(out=w_half[:, t : t + step, :], in_=src[:, t : t + step, :])
             w_raw[half] = w_half
 
-        load_x(0, 1)
-        load_w(0, pieces=2)
-        load_x(1, 2)
-        load_x(2, 4)
-        load_x(4, 7)
-        load_w(1)
-        load_w(2)
-        load_w(3)
-        load_c(0, 4)
-        load_c(4, 7)
-        load_w(4)
+        for kind, a, b in [['x', 0, 1], ['w', 0, 2], ['x', 1, 2], ['x', 2, 4], ['x', 4, 7], ['w', 1, 1], ['w', 2, 1], ['w', 3, 1], ['c', 0, 4], ['c', 4, 7], ['w', 4, 1]]:
+            if kind == "x":
+                load_x(a, b)
+            elif kind == "c":
+                load_c(a, b)
+            else:
+                load_w(a, b)
 
         ident = const.tile([P, P], F32, name="ident")
         make_identity(nc, ident[:])
@@ -77,14 +73,19 @@ def tile_infonceloss_pa_kernel(tc, embeddings, contexts, W, out):
         nc.vector.memset(warm[:], 1.0)
         nc.scalar.activation(out=warm[:, 1:2], in_=warm[:, 0:1], func=ACT.Exp)
         mask8 = const.tile([P, B_LO], F32, name="mask8")
-        nc.vector.tensor_reduce(
-            out=mask8[:], in_=ident[:].rearrange("p (q l) -> p l q", l=B_LO), axis=AX.X, op=ALU.add
-        )
         fold = const.tile([P, P], F32, name="fold")
-        nc.vector.memset(fold[:], 0.0)
-        nc.vector.tensor_reduce(
-            out=fold[:, 0:B_HI], in_=ident[:].rearrange("p (q l) -> p q l", l=B_LO), axis=AX.X, op=ALU.add
-        )
+        mask_s = const.tile([P, N_STEP, B_LO], F32, name="mask_s")
+
+        def masks():
+            nc.vector.tensor_reduce(
+                out=mask8[:], in_=ident[:].rearrange("p (q l) -> p l q", l=B_LO), axis=AX.X, op=ALU.add
+            )
+            nc.vector.memset(fold[:], 0.0)
+            nc.vector.tensor_reduce(
+                out=fold[:, 0:B_HI], in_=ident[:].rearrange("p (q l) -> p q l", l=B_LO), axis=AX.X, op=ALU.add
+            )
+            for k in range(N_STEP):
+                nc.vector.tensor_scalar(out=mask_s[:, k, :], in0=mask8[:], scalar1=1.0 / (P * (N_SLICE - k)), scalar2=None, op0=ALU.mult)
 
         xq = keep.tile([P, N_SLICE, TILE_WORDS], U32, name="xq", align_bytes=64)
         xs = keep.tile([P, N_SLICE, TILE_WORDS], U8, name="xs", align_bytes=64)
@@ -106,13 +107,12 @@ def tile_infonceloss_pa_kernel(tc, embeddings, contexts, W, out):
         def quantise(codes, scales, values):
             nc.vector.quantize_mx(out=flat(codes).bitcast(FP8X4), scales=flat(scales), in_=flat(values))
 
-        def quantise_tiles(grp, n, codes, scales, widest):
+        def quantise_tiles(grp, n, codes, scales):
             i0 = 0
             for w in (4, 2, 1):
-                if w <= widest:
-                    for call in range((n - i0) // w):
-                        quantise(codes[:, i0 : i0 + w, :], scales[:, i0 : i0 + w, :], grp[:, i0 : i0 + w, :])
-                        i0 += w
+                for call in range((n - i0) // w):
+                    quantise(codes[:, i0 : i0 + w, :], scales[:, i0 : i0 + w, :], grp[:, i0 : i0 + w, :])
+                    i0 += w
 
         def split_words(raw_tiles, n):
             split = split_pool.tile([P, 4, FEAT], BF16, name="split", tag="split")
@@ -120,13 +120,13 @@ def tile_infonceloss_pa_kernel(tc, embeddings, contexts, W, out):
                 out=flat(split[:, 0:n, :]).bitcast(F32).rearrange("p (a u r) -> p a u r", u=2, r=P),
                 in_=flat(raw_tiles).bitcast(F32).rearrange("p (a r u) -> p a u r", u=2, r=P),
             )
-            return [split[:, i, :] for i in range(n)]
+            return split[:, 0:n, :]
 
-        def transposes(rows, is_split, on_vector):
+        def transposes(rows, n, is_split, on_vector):
             grp = grp_pool.tile([P, 4, FEAT], BF16, name="grp", tag="grp", align_bytes=64)
-            for i in range(len(rows)):
+            for i in range(n):
                 bank = ring.tile([P, 4, P], F32, name="bank", tag="bank")
-                words = rows[i].bitcast(F32)
+                words = rows[:, i, :].bitcast(F32)
                 for j in range(4):
                     g, u = j // 2, j % 2
                     if is_split:
@@ -148,14 +148,15 @@ def tile_infonceloss_pa_kernel(tc, embeddings, contexts, W, out):
             if kind == "c":
                 return c_raw[:, a:b, :], b - a, cq[:, a:b, :], cs[:, a:b, :]
             k, g = a // 2, a % 2
-            tiles = slice(4 * g, 4 * g + 4)
-            return w_raw[a][:], 4, wq[k][:, tiles, :], ws[k][:, tiles, :]
+            t0, t1 = {0: (0, 4), 1: (0, 2), 2: (2, 4)}[b]
+            tiles = slice(4 * g + t0, 4 * g + t1)
+            return w_raw[a][:, t0:t1, :], t1 - t0, wq[k][:, tiles, :], ws[k][:, tiles, :]
 
         def xw_row(k, g2, s):
             return 2 * GROUP0[k] + g2 * (N_SLICE - k) + s
 
         def stage1(k, g2, slices):
-            xwg = xwg_pool.tile([P, 2, 512], BF16, name="xwg", tag="xwg", align_bytes=64)
+            xwg = xwg_pool.tile([P, 4, 512], BF16, name="xwg", tag="xwg", align_bytes=64)
             for i in range(len(slices)):
                 s = slices[i]
                 bank = ring.tile([P, 4, P], F32, name="bank", tag="bank")
@@ -171,7 +172,8 @@ def tile_infonceloss_pa_kernel(tc, embeddings, contexts, W, out):
                             start=(g1 == 0),
                             stop=(g1 == 1),
                         )
-                nc.scalar.copy(
+                copy = nc.vector.tensor_copy if (k, g2, s) in XV else nc.scalar.copy
+                copy(
                     out=xwg[:, i, :].rearrange("p (b t) -> p b t", t=4),
                     in_=bank[:].rearrange("p t b -> p b t"),
                 )
@@ -180,186 +182,183 @@ def tile_infonceloss_pa_kernel(tc, embeddings, contexts, W, out):
         def quantise_xw(k, g2, slices, xwg):
             n = len(slices)
             r0 = xw_row(k, g2, slices[0])
-            quantise(xwq[:, r0 : r0 + n, :], xws[:, r0 : r0 + n, :], xwg[:, 0:n, :])
+            i0 = 0
+            for w in (4, 2, 1):
+                for call in range((n - i0) // w):
+                    quantise(xwq[:, r0 + i0 : r0 + i0 + w, :], xws[:, r0 + i0 : r0 + i0 + w, :], xwg[:, i0 : i0 + w, :])
+                    i0 += w
 
-        score_banks = {}
+        pairs = [(k, s) for k in range(N_STEP) for s in range(N_SLICE - k)]
+        score_bank = {}
 
-        def scores(k, first_slices):
-            n_s = N_SLICE - k
-            score_banks[k] = []
-            for j in range(len(first_slices)):
-                s0 = first_slices[j]
-                n = (first_slices[j + 1] if j + 1 < len(first_slices) else n_s) - s0
+        def scores(p0, p1):
+            if p0 == 24:
+                sc = ring.tile([P, 4, P], F32, name="sc_last", tag="bank")
+            else:
                 sc = scp.tile([P, 4, P], F32, name="sc", tag="sc")
-                for i in range(n):
-                    for g2 in range(2):
-                        r = xw_row(k, g2, s0 + i)
-                        cols = slice(P * g2, P * (g2 + 1))
-                        nc.tensor.matmul_mx(
-                            out=sc[:, i, :],
-                            lhsT=xwq[:, r, :].bitcast(FP8X4),
-                            lhsT_scale=xws[:, r, :],
-                            rhs=cq[:, s0 + i, cols].bitcast(FP8X4),
-                            rhs_scale=cs[:, s0 + i, cols],
-                            start=(g2 == 0),
-                            stop=(g2 == 1),
-                        )
-                score_banks[k].append((sc, GROUP0[k] + s0, n))
+            for i in range(p1 - p0):
+                k, s = pairs[p0 + i]
+                for g2 in range(2):
+                    r = xw_row(k, g2, s)
+                    cols = slice(P * g2, P * (g2 + 1))
+                    nc.tensor.matmul_mx(
+                        out=sc[:, i, :],
+                        lhsT=xwq[:, r, :].bitcast(FP8X4),
+                        lhsT_scale=xws[:, r, :],
+                        rhs=cq[:, s, cols].bitcast(FP8X4),
+                        rhs_scale=cs[:, s, cols],
+                        start=(g2 == 0),
+                        stop=(g2 == 1),
+                    )
+                score_bank[p0 + i] = sc[:, i, :]
+            score_bank["bank", p0] = sc
 
-        def row_max(k, b):
-            sc, gi, n = score_banks[k][b]
-            nc.vector.tensor_reduce(out=negmax[:, gi : gi + n], in_=sc[:, 0:n, :], axis=AX.X, op=ALU.max, negate=True)
+        def row_max(p0, p1):
+            sc = score_bank["bank", p0]
+            nc.vector.tensor_reduce(out=negmax[:, p0:p1], in_=sc[:, 0 : p1 - p0, :], axis=AX.X, op=ALU.max, negate=True)
 
-        def diagonal(k, b):
-            sc, gi, n = score_banks[k][b]
-            for i in range(n):
+        def diagonal(p0, p1):
+            for p in range(p0, p1):
                 jv = junk.tile([P, P], F32, name="jv", tag="jv")
                 nc.vector.scalar_tensor_tensor(
                     out=jv[:],
-                    in0=sc[:, i, :],
-                    scalar=negmax[:, gi + i : gi + i + 1],
+                    in0=score_bank[p],
+                    scalar=negmax[:, p : p + 1],
                     in1=ident[:],
                     op0=ALU.add,
                     op1=ALU.mult,
-                    accum_out=dm[:, gi + i : gi + i + 1],
+                    accum_out=dm[:, p : p + 1],
                 )
 
-        def exponentials(k, b):
-            sc, gi, n = score_banks[k][b]
-            for i in range(n):
+        def exponentials(p0, p1):
+            for p in range(p0, p1):
                 js = junk.tile([P, P], F32, name="js", tag="js")
                 nc.scalar.activation(
                     out=js[:],
-                    in_=sc[:, i, :],
+                    in_=score_bank[p],
                     func=ACT.Exp,
-                    bias=negmax[:, gi + i : gi + i + 1],
+                    bias=negmax[:, p : p + 1],
                     scale=1.0,
-                    accum_out=sumexp[:, gi + i : gi + i + 1],
+                    accum_out=sumexp[:, p : p + 1],
                 )
 
         def step_columns(tile, k):
             g0 = GROUP0[k]
             return tile[:, B_LO * g0 : B_LO * (g0 + N_SLICE - k)].rearrange("p (l s) -> p l s", l=B_LO)
 
-        def spread_diagonal(k):
+        def spread_diagonal(k, engine):
             n_s = N_SLICE - k
             shape = [P, B_LO, n_s]
-            nc.vector.tensor_tensor(
+            engine.tensor_tensor(
                 out=step_columns(spread_d, k),
                 in0=dm[:, GROUP0[k] : GROUP0[k] + n_s].unsqueeze(1).to_broadcast(shape),
                 in1=mask8[:].unsqueeze(2).to_broadcast(shape),
                 op=ALU.mult,
             )
 
-        def spread_sum(k):
+        def spread_sum(k, engine):
             n_s = N_SLICE - k
             shape = [P, B_LO, n_s]
-            nc.vector.scalar_tensor_tensor(
+            engine.tensor_tensor(
                 out=step_columns(spread_s, k),
                 in0=sumexp[:, GROUP0[k] : GROUP0[k] + n_s].unsqueeze(1).to_broadcast(shape),
-                scalar=1.0 / (P * n_s),
-                in1=mask8[:].unsqueeze(2).to_broadcast(shape),
-                op0=ALU.mult,
-                op1=ALU.mult,
+                in1=mask_s[:, k, :].unsqueeze(2).to_broadcast(shape),
+                op=ALU.mult,
             )
 
-        chunks = []
-        last_chunk = []
-        for k in range(N_STEP):
-            for g2 in range(2):
-                for s in range(0, N_SLICE - k, 2):
-                    chunks.append((k, g2, list(range(s, min(s + 2, N_SLICE - k)))))
-            last_chunk.append(len(chunks) - 1)
-        groups = [[("x", 0, 1), ("w", 0, 0), ("x", 1, 2), ("x", 2, 4)], [("x", 4, 7)], [("w", 1, 0)], [("w", 2, 0)]]
-        groups += [[("w", 3, 0)], [("c", 0, 4)], [("c", 4, 7)]] + [[("w", half, 0)] for half in range(4, 2 * N_STEP)]
-        contexts_ready = 12
-        scores_before = [max(last_chunk[k] + 3, contexts_ready) for k in range(N_STEP - 1)]
-        n_groups = 0
-        split_rows = {}
+        chunks = [[0, 0, [0, 1, 2, 3]], [0, 0, [4, 5, 6]], [0, 1, [0, 1, 2, 3]], [0, 1, [4, 5, 6]], [1, 0, [0, 1, 2, 3]], [1, 0, [4, 5]], [1, 1, [0, 1, 2, 3]], [1, 1, [4, 5]], [2, 0, [0, 1, 2]], [2, 0, [3, 4]], [2, 1, [0, 1, 2]], [2, 1, [3, 4]], [3, 0, [0, 1, 2, 3]], [3, 1, [0, 1, 2, 3]], [4, 0, [0, 1, 2]], [4, 1, [0, 1]], [4, 1, [2]]]
 
-        def split_group(i):
-            for kind, a, b in groups[i]:
-                raw_tiles, n = operand(kind, a, b)[0:2]
-                split_rows[i] = split_words(raw_tiles, n)
-                if kind == "w" and a + W_BUFFERS < 2 * N_STEP:
-                    load_w(a + W_BUFFERS)
+        XV = []
+        HEAD = [['x', 0, 1, False, [0]], ['w', 0, 1, False, [1]], ['w', 0, 2, False, [1]], ['x', 1, 2, False, [0]], ['x', 2, 4, False, [1]]]
+        GROUPS = {0: [['x', 4, 7, False, [2]]], 1: [['w', 1, 0, True, [1, 3]]], 2: [['w', 2, 0, False, [3]]], 3: [['w', 3, 0, True, [1, 3]]], 4: [['c', 0, 4, True, [1, 3]]], 5: [['c', 4, 7, True, [0, 2]]], 6: [['w', 4, 0, False, [3]]], 7: [['w', 5, 0, True, [1, 3]]], 8: [['w', 6, 0, False, [3]]], 9: [['w', 7, 0, True, [1, 3]]], 11: [['w', 8, 0, False, [3]]], 12: [['w', 9, 0, True, [1, 3]]]}
+        JOBS = {6: [['scores', 0, 4], ['max', 0, 4]], 7: [['exp', 0, 4], ['diag', 0, 4]], 8: [['scores', 4, 8], ['max', 4, 8]], 9: [['exp', 4, 8], ['diag', 4, 8]], 10: [['scores', 8, 12], ['max', 8, 12]], 11: [['exp', 8, 12], ['diag', 8, 12], ['spread', 0]], 13: [['scores', 12, 16], ['max', 12, 16]], 14: [['exp', 12, 16], ['diag', 12, 16], ['scores', 16, 18], ['max', 16, 18]], 15: [['exp', 16, 18], ['diag', 16, 18], ['scores', 18, 22], ['max', 18, 22]], 16: [['spread', 1], ['spread', 2]]}
+        EARLY = 3
+        ready = {}
+        def prepare(grp_spec):
+            kind, a, b, is_split, on_v = grp_spec
+            raw_tiles, n, codes, scales = operand(kind, a, b)
+            ready[kind, a, b] = split_words(raw_tiles, n) if is_split else raw_tiles
+            if is_split:
+                reload(grp_spec)
 
-        unquantised = None
-        step = -1
-        since = 0
+        def reload(grp_spec):
+            kind, a, b = grp_spec[0:3]
+            if kind == "w" and b != 1 and a + W_BUFFERS < 2 * N_STEP:
+                load_w(a + W_BUFFERS)
+
+        def turn(grp_spec):
+            kind, a, b, is_split, on_v = grp_spec
+            raw_tiles, n, codes, scales = operand(kind, a, b)
+            grp = transposes(ready[kind, a, b], n, is_split, on_v)
+            if not is_split:
+                reload(grp_spec)
+            return grp, n, codes, scales
+
+        waiting = []
+        prepare(HEAD[0])
+        for i in range(len(HEAD)):
+            if i + 1 < len(HEAD):
+                prepare(HEAD[i + 1])
+            waiting.append(turn(HEAD[i]))
+            if i >= 1:
+                quantise_tiles(*waiting.pop(0))
+        masks()
+        order = sorted(GROUPS)
+        flatg = [g for j in order for g in GROUPS[j]]
+        n_prep = 0
+        n_turn = 0
+        unquantised = []
         for j in range(len(chunks)):
             staged = []
-            if n_groups < len(groups) and (j < 2 or j % 2 == 0):
-                for kind, a, b in groups[n_groups]:
-                    raw_tiles, n, codes, scales = operand(kind, a, b)
-                    if j == 0:
-                        grp = transposes([raw_tiles[:, i, :] for i in range(n)], False, (0, 2))
-                        quantise_tiles(grp, n, codes, scales, 2)
-                        if kind == "w":
-                            load_w(a + W_BUFFERS)
-                    else:
-                        grp = transposes(split_rows[n_groups], True, (3,) if kind == "w" else (1, 3))
-                        staged.append((grp, n, codes, scales))
-                n_groups += 1
-            if unquantised is not None:
-                quantise_xw(unquantised[0], unquantised[1], unquantised[2], unquantised[3])
-            for grp, n, codes, scales in staged:
-                quantise_tiles(grp, n, codes, scales, 4)
-            since += 1
-            if j in scores_before:
-                step += 1
-                since = 0
-                scores(step, (0, 4) if N_SLICE - step > 4 else (0,))
+            for g in GROUPS.get(j, []):
+                while n_prep < min(n_turn + 1, len(flatg)):
+                    prepare(flatg[n_prep])
+                    n_prep += 1
+                staged.append(turn(g))
+                n_turn += 1
+            while n_prep < min(n_turn + 2, len(flatg)) and GROUPS.get(j, []):
+                prepare(flatg[n_prep])
+                n_prep += 1
+            for job in JOBS.get(j, []):
+                if job[0] == "scores":
+                    scores(job[1], job[2])
+                if job[0] == "exp":
+                    exponentials(job[1], job[2])
+            while len(unquantised) > 0:
+                quantise_xw(*unquantised.pop(0))
+            for w in waiting:
+                quantise_tiles(*w)
+            waiting = []
+            for w in staged:
+                quantise_tiles(*w)
             k, g2, slices = chunks[j]
-            unquantised = (k, g2, slices, stage1(k, g2, slices))
-            if step >= 0:
-                two_banks = len(score_banks[step]) > 1
-                if since == 0:
-                    row_max(step, 0)
-                    diagonal(step, 0)
-                if since == 1:
-                    exponentials(step, 0)
-                    if two_banks:
-                        row_max(step, 1)
-                        diagonal(step, 1)
-                if since == 2 and two_banks:
-                    exponentials(step, 1)
-                if since == 3:
-                    spread_diagonal(step)
-                    spread_sum(step)
-            if j < 2 or j % 2 == 0:
-                if j == 0:
-                    split_group(1)
-                if n_groups + 1 < len(groups):
-                    split_group(n_groups + 1)
-        quantise_xw(unquantised[0], unquantised[1], unquantised[2], unquantised[3])
-
+            unquantised.append((k, g2, slices, stage1(k, g2, slices)))
+            for job in JOBS.get(j, []):
+                if job[0] == "max":
+                    row_max(job[1], job[2])
+                if job[0] == "diag":
+                    diagonal(job[1], job[2])
+                if job[0] == "spread":
+                    spread_diagonal(job[1], nc.gpsimd)
+                    spread_sum(job[1], nc.gpsimd)
         last = N_STEP - 1
         n_col = B_LO * N_GROUP
         n_early = B_LO * GROUP0[last]
-        scores(last, (0, 2))
-        row_max(last, 0)
-        row_max(last, 1)
-        exponentials(last, 0)
-        exponentials(last, 1)
-        nc.scalar.activation(out=warm[:, 1:2], in_=sumexp[:, N_GROUP - 1 : N_GROUP], func=ACT.Ln)
-        spread_diagonal(last - 1)
-        spread_sum(last - 1)
+        lnz = keep.tile([P, n_col], F32, name="lnz")
+        res = keep.tile([P, n_col], F32, name="res")
         zs = ring.tile([P, 512], F32, name="zs", tag="bank")
         zd = ring.tile([P, 512], F32, name="zd", tag="bank")
-        nc.tensor.matmul(zs[:, 0:n_early], lhsT=fold[:], rhs=spread_s[:, 0:n_early], start=True, stop=True)
-        nc.tensor.matmul(zd[:, 0:n_early], lhsT=fold[:], rhs=spread_d[:, 0:n_early], start=True, stop=True)
-        spread_sum(last)
-        nc.tensor.matmul(zs[:, n_early:n_col], lhsT=fold[:], rhs=spread_s[:, n_early:n_col], start=True, stop=True)
-        diagonal(last, 0)
-        diagonal(last, 1)
-        spread_diagonal(last)
-        nc.tensor.matmul(zd[:, n_early:n_col], lhsT=fold[:], rhs=spread_d[:, n_early:n_col], start=True, stop=True)
-        lnz = keep.tile([P, n_col], F32, name="lnz")
-        nc.scalar.activation(out=lnz[0:B_HI, :], in_=zs[0:B_HI, 0:n_col], func=ACT.Ln)
-        res = keep.tile([P, n_col], F32, name="res")
-        nc.vector.tensor_tensor(out=res[0:B_HI, :], in0=lnz[0:B_HI, :], in1=zd[0:B_HI, 0:n_col], op=ALU.subtract)
-        for k in range(N_STEP):
+        zs2 = ring.tile([P, 512], F32, name="zs2", tag="bank")
+        zd2 = ring.tile([P, 512], F32, name="zd2", tag="bank")
+
+        def folded(tile, src, c0, c1):
+            nc.tensor.matmul(tile[:, 0 : c1 - c0], lhsT=fold[:], rhs=src[:, c0:c1], start=True, stop=True)
+
+        def loss(zs, zd, c0, c1):
+            nc.scalar.activation(out=lnz[0:B_HI, c0:c1], in_=zs[0:B_HI, 0 : c1 - c0], func=ACT.Ln)
+            nc.vector.tensor_tensor(out=res[0:B_HI, c0:c1], in0=lnz[0:B_HI, c0:c1], in1=zd[0:B_HI, 0 : c1 - c0], op=ALU.subtract)
+
+        def store(k):
             n_s = N_SLICE - k
             g0 = GROUP0[k]
             queue = nc.sync if k % 2 == 0 else nc.scalar
@@ -367,3 +366,29 @@ def tile_infonceloss_pa_kernel(tc, embeddings, contexts, W, out):
                 out=out[P * g0 : P * (g0 + n_s)].rearrange("(q c) -> q c", q=B_HI),
                 in_=res[0:B_HI, B_LO * g0 : B_LO * (g0 + n_s)],
             )
+
+        exponentials(18, 22)
+        scores(22, 24)
+        row_max(22, 24)
+        for u in unquantised:
+            quantise_xw(*u)
+        scores(24, 25)
+        row_max(24, 25)
+        exponentials(22, 24)
+        exponentials(24, 25)
+        nc.scalar.activation(out=warm[:, 1:2], in_=sumexp[:, N_GROUP - 1 : N_GROUP], func=ACT.Ln)
+        diagonal(18, 22)
+        for k in range(EARLY, last):
+            spread_diagonal(k, nc.gpsimd)
+            spread_sum(k, nc.gpsimd)
+        spread_sum(last, nc.vector)
+        folded(zs2, spread_s, n_early, n_col)
+        folded(zs, spread_s, 0, n_early)
+        diagonal(22, 25)
+        folded(zd, spread_d, 0, n_early)
+        spread_diagonal(last, nc.vector)
+        folded(zd2, spread_d, n_early, n_col)
+        loss(zs, zd, 0, n_early)
+        loss(zs2, zd2, n_early, n_col)
+        for k in range(N_STEP):
+            store(k)

@@ -74,7 +74,7 @@ def tile_infonceloss_pa_kernel(tc, embeddings, contexts, W, out):
         nc.scalar.activation(out=warm[:, 1:2], in_=warm[:, 0:1], func=ACT.Exp)
         mask8 = const.tile([P, B_LO], F32, name="mask8")
         fold = const.tile([P, P], F32, name="fold")
-        mask_s = const.tile([P, N_STEP, B_LO], F32, name="mask_s")
+        mask_s = const.tile([P, B_LO, N_GROUP], F32, name="mask_s")
 
         def masks():
             nc.vector.tensor_reduce(
@@ -85,7 +85,14 @@ def tile_infonceloss_pa_kernel(tc, embeddings, contexts, W, out):
                 out=fold[:, 0:B_HI], in_=ident[:].rearrange("p (q l) -> p q l", l=B_LO), axis=AX.X, op=ALU.add
             )
             for k in range(N_STEP):
-                nc.vector.tensor_scalar(out=mask_s[:, k, :], in0=mask8[:], scalar1=1.0 / (P * (N_SLICE - k)), scalar2=None, op0=ALU.mult)
+                n_s = N_SLICE - k
+                nc.vector.tensor_scalar(
+                    out=mask_s[:, :, GROUP0[k] : GROUP0[k] + n_s],
+                    in0=mask8[:].unsqueeze(2).to_broadcast([P, B_LO, n_s]),
+                    scalar1=1.0 / (P * n_s),
+                    scalar2=None,
+                    op0=ALU.mult,
+                )
 
         xq = keep.tile([P, N_SLICE, TILE_WORDS], U32, name="xq", align_bytes=64)
         xs = keep.tile([P, N_SLICE, TILE_WORDS], U8, name="xs", align_bytes=64)
@@ -98,8 +105,6 @@ def tile_infonceloss_pa_kernel(tc, embeddings, contexts, W, out):
         negmax = keep.tile([P, N_GROUP], F32, name="negmax")
         sumexp = keep.tile([P, N_GROUP], F32, name="sumexp")
         dm = keep.tile([P, N_GROUP], F32, name="dm")
-        spread_s = keep.tile([P, B_LO * N_GROUP], F32, name="spread_s")
-        spread_d = keep.tile([P, B_LO * N_GROUP], F32, name="spread_d")
 
         def flat(ap):
             return ap.rearrange("p i c -> p (i c)")
@@ -242,37 +247,35 @@ def tile_infonceloss_pa_kernel(tc, embeddings, contexts, W, out):
                     accum_out=sumexp[:, p : p + 1],
                 )
 
-        def step_columns(tile, k):
-            g0 = GROUP0[k]
-            return tile[:, B_LO * g0 : B_LO * (g0 + N_SLICE - k)].rearrange("p (l s) -> p l s", l=B_LO)
-
-        def spread_diagonal(k, engine):
-            n_s = N_SLICE - k
-            shape = [P, B_LO, n_s]
-            engine.tensor_tensor(
-                out=step_columns(spread_d, k),
-                in0=dm[:, GROUP0[k] : GROUP0[k] + n_s].unsqueeze(1).to_broadcast(shape),
-                in1=mask8[:].unsqueeze(2).to_broadcast(shape),
+        def spread(p0, p1, values, mask, name):
+            n = p1 - p0
+            tile = keep.tile([P, B_LO, n], F32, name=name)
+            nc.vector.tensor_tensor(
+                out=tile[:],
+                in0=values[:, p0:p1].unsqueeze(1).to_broadcast([P, B_LO, n]),
+                in1=mask,
                 op=ALU.mult,
             )
+            return tile[:].rearrange("p l s -> p (l s)")
 
-        def spread_sum(k, engine):
-            n_s = N_SLICE - k
-            shape = [P, B_LO, n_s]
-            engine.tensor_tensor(
-                out=step_columns(spread_s, k),
-                in0=sumexp[:, GROUP0[k] : GROUP0[k] + n_s].unsqueeze(1).to_broadcast(shape),
-                in1=mask_s[:, k, :].unsqueeze(2).to_broadcast(shape),
-                op=ALU.mult,
-            )
+        def spread_sum(p0, p1, name):
+            return spread(p0, p1, sumexp, mask_s[:, :, p0:p1], name)
+
+        def spread_diagonal(p0, p1, name):
+            return spread(p0, p1, dm, mask8[:].unsqueeze(2).to_broadcast([P, B_LO, p1 - p0]), name)
+
+        def folded(src, n, name):
+            tile = ring.tile([P, 512], F32, name=name, tag="bank")
+            nc.tensor.matmul(tile[:, 0:n], lhsT=fold[:], rhs=src, start=True, stop=True)
+            return tile
 
         chunks = [[0, 0, [0, 1, 2, 3]], [0, 0, [4, 5, 6]], [0, 1, [0, 1, 2, 3]], [0, 1, [4, 5, 6]], [1, 0, [0, 1, 2, 3]], [1, 0, [4, 5]], [1, 1, [0, 1, 2, 3]], [1, 1, [4, 5]], [2, 0, [0, 1, 2]], [2, 0, [3, 4]], [2, 1, [0, 1, 2]], [2, 1, [3, 4]], [3, 0, [0, 1, 2, 3]], [3, 1, [0, 1, 2, 3]], [4, 0, [0, 1, 2]], [4, 1, [0, 1]], [4, 1, [2]]]
 
-        XV = []
-        HEAD = [['x', 0, 1, False, [0]], ['w', 0, 1, False, [1]], ['w', 0, 2, False, [1]], ['x', 1, 2, False, [0]], ['x', 2, 4, False, [1]]]
-        GROUPS = {0: [['x', 4, 7, False, [2]]], 1: [['w', 1, 0, True, [1, 3]]], 2: [['w', 2, 0, False, [3]]], 3: [['w', 3, 0, True, [1, 3]]], 4: [['c', 0, 4, True, [1, 3]]], 5: [['c', 4, 7, True, [0, 2]]], 6: [['w', 4, 0, False, [3]]], 7: [['w', 5, 0, True, [1, 3]]], 8: [['w', 6, 0, False, [3]]], 9: [['w', 7, 0, True, [1, 3]]], 11: [['w', 8, 0, False, [3]]], 12: [['w', 9, 0, True, [1, 3]]]}
-        JOBS = {6: [['scores', 0, 4], ['max', 0, 4]], 7: [['exp', 0, 4], ['diag', 0, 4]], 8: [['scores', 4, 8], ['max', 4, 8]], 9: [['exp', 4, 8], ['diag', 4, 8]], 10: [['scores', 8, 12], ['max', 8, 12]], 11: [['exp', 8, 12], ['diag', 8, 12], ['spread', 0]], 13: [['scores', 12, 16], ['max', 12, 16]], 14: [['exp', 12, 16], ['diag', 12, 16], ['scores', 16, 18], ['max', 16, 18]], 15: [['exp', 16, 18], ['diag', 16, 18], ['scores', 18, 22], ['max', 18, 22]], 16: [['spread', 1], ['spread', 2]]}
-        EARLY = 3
+        XV = [(3, 0, 0), (3, 1, 0), (4, 0, 0)]
+        HEAD = [['x', 0, 1, False, []], ['w', 0, 1, True, []], ['w', 0, 2, True, []], ['x', 1, 2, True, []], ['x', 2, 4, True, []]]
+        GROUPS = {0: [['x', 4, 7, False, [2]]], 1: [['w', 1, 0, True, [3]]], 2: [['w', 2, 0, False, [3]]], 3: [['w', 3, 0, True, [3]]], 4: [['c', 0, 4, True, [1, 3]], ['c', 4, 7, True, [0, 2]]], 5: [['w', 4, 0, False, [3]]], 6: [['w', 5, 0, True, [3]]], 7: [['w', 6, 0, False, [3]]], 8: [['w', 7, 0, True, [3]]], 9: [['w', 8, 0, False, [3]]], 10: [['w', 9, 0, True, [3]]]}
+        JOBS = {6: [['scores', 0, 4], ['max', 0, 4]], 7: [['exp', 0, 4], ['diag', 0, 4]], 8: [['scores', 4, 8], ['max', 4, 8]], 9: [['exp', 4, 8], ['diag', 4, 8]], 10: [['scores', 8, 12], ['max', 8, 12]], 11: [['exp', 8, 12], ['diag', 8, 12]], 12: [['scores', 12, 16], ['max', 12, 16]], 13: [['exp', 12, 16], ['diag', 12, 16]], 14: [['scores', 16, 18], ['max', 16, 18]], 15: [['exp', 16, 18], ['diag', 16, 18], ['scores', 18, 22], ['max', 18, 22]]}
+        SPLIT_AT = 18
         ready = {}
         def prepare(grp_spec):
             kind, a, b, is_split, on_v = grp_spec
@@ -324,6 +327,9 @@ def tile_infonceloss_pa_kernel(tc, embeddings, contexts, W, out):
                     scores(job[1], job[2])
                 if job[0] == "exp":
                     exponentials(job[1], job[2])
+            for job in JOBS.get(j, []):
+                if job[0] == "max0":
+                    row_max(job[1], job[2])
             while len(unquantised) > 0:
                 quantise_xw(*unquantised.pop(0))
             for w in waiting:
@@ -338,25 +344,19 @@ def tile_infonceloss_pa_kernel(tc, embeddings, contexts, W, out):
                     row_max(job[1], job[2])
                 if job[0] == "diag":
                     diagonal(job[1], job[2])
-                if job[0] == "spread":
-                    spread_diagonal(job[1], nc.gpsimd)
-                    spread_sum(job[1], nc.gpsimd)
-        last = N_STEP - 1
-        n_col = B_LO * N_GROUP
-        n_early = B_LO * GROUP0[last]
-        lnz = keep.tile([P, n_col], F32, name="lnz")
-        res = keep.tile([P, n_col], F32, name="res")
-        zs = ring.tile([P, 512], F32, name="zs", tag="bank")
-        zd = ring.tile([P, 512], F32, name="zd", tag="bank")
-        zs2 = ring.tile([P, 512], F32, name="zs2", tag="bank")
-        zd2 = ring.tile([P, 512], F32, name="zd2", tag="bank")
+        lnz = keep.tile([P, B_LO * N_GROUP], F32, name="lnz")
+        res = [keep.tile([P, B_LO, N_SLICE - k], F32, name="res%d" % k) for k in range(N_STEP)]
 
-        def folded(tile, src, c0, c1):
-            nc.tensor.matmul(tile[:, 0 : c1 - c0], lhsT=fold[:], rhs=src[:, c0:c1], start=True, stop=True)
-
-        def loss(zs, zd, c0, c1):
-            nc.scalar.activation(out=lnz[0:B_HI, c0:c1], in_=zs[0:B_HI, 0 : c1 - c0], func=ACT.Ln)
-            nc.vector.tensor_tensor(out=res[0:B_HI, c0:c1], in0=lnz[0:B_HI, c0:c1], in1=zd[0:B_HI, 0 : c1 - c0], op=ALU.subtract)
+        def loss(zs, zd, p0, p1, steps):
+            n = p1 - p0
+            ln = lnz[0:B_HI, B_LO * p0 : B_LO * p1]
+            nc.scalar.activation(out=ln, in_=zs[0:B_HI, 0 : B_LO * n], func=ACT.Ln)
+            ln = ln.rearrange("q (l s) -> q l s", l=B_LO)
+            dg = zd[0:B_HI, 0 : B_LO * n].rearrange("q (l s) -> q l s", l=B_LO)
+            for k in steps:
+                s0 = GROUP0[k] - p0
+                s1 = s0 + N_SLICE - k
+                nc.vector.tensor_tensor(out=res[k][0:B_HI, :, :], in0=ln[:, :, s0:s1], in1=dg[:, :, s0:s1], op=ALU.subtract)
 
         def store(k):
             n_s = N_SLICE - k
@@ -364,7 +364,7 @@ def tile_infonceloss_pa_kernel(tc, embeddings, contexts, W, out):
             queue = nc.sync if k % 2 == 0 else nc.scalar
             queue.dma_start(
                 out=out[P * g0 : P * (g0 + n_s)].rearrange("(q c) -> q c", q=B_HI),
-                in_=res[0:B_HI, B_LO * g0 : B_LO * (g0 + n_s)],
+                in_=res[k][0:B_HI, :, :].rearrange("q l s -> q (l s)"),
             )
 
         exponentials(18, 22)
@@ -373,22 +373,24 @@ def tile_infonceloss_pa_kernel(tc, embeddings, contexts, W, out):
         for u in unquantised:
             quantise_xw(*u)
         scores(24, 25)
+
         row_max(24, 25)
         exponentials(22, 24)
         exponentials(24, 25)
         nc.scalar.activation(out=warm[:, 1:2], in_=sumexp[:, N_GROUP - 1 : N_GROUP], func=ACT.Ln)
-        diagonal(18, 22)
-        for k in range(EARLY, last):
-            spread_diagonal(k, nc.gpsimd)
-            spread_sum(k, nc.gpsimd)
-        spread_sum(last, nc.vector)
-        folded(zs2, spread_s, n_early, n_col)
-        folded(zs, spread_s, 0, n_early)
-        diagonal(22, 25)
-        folded(zd, spread_d, 0, n_early)
-        spread_diagonal(last, nc.vector)
-        folded(zd2, spread_d, n_early, n_col)
-        loss(zs, zd, 0, n_early)
-        loss(zs2, zd2, n_early, n_col)
-        for k in range(N_STEP):
+
+        early_s = spread_sum(0, SPLIT_AT, "spread_s0")
+        early_d = spread_diagonal(0, SPLIT_AT, "spread_d0")
+        zs0 = folded(early_s, B_LO * SPLIT_AT, "zs0")
+        zd0 = folded(early_d, B_LO * SPLIT_AT, "zd0")
+        late_s = spread_sum(SPLIT_AT, N_GROUP, "spread_s1")
+        zs1 = folded(late_s, B_LO * (N_GROUP - SPLIT_AT), "zs1")
+        diagonal(18, 22); diagonal(22, 25)
+        late_d = spread_diagonal(SPLIT_AT, N_GROUP, "spread_d1")
+        zd1 = folded(late_d, B_LO * (N_GROUP - SPLIT_AT), "zd1")
+        loss(zs0, zd0, 0, SPLIT_AT, range(3))
+        for k in range(3):
+            store(k)
+        loss(zs1, zd1, SPLIT_AT, N_GROUP, range(3, N_STEP))
+        for k in range(3, N_STEP):
             store(k)

@@ -272,9 +272,9 @@ def tile_infonceloss_pa_kernel(tc, embeddings, contexts, W, out):
         chunks = [[0, 0, [0, 1, 2, 3]], [0, 0, [4, 5, 6]], [0, 1, [0, 1, 2, 3]], [0, 1, [4, 5, 6]], [1, 0, [0, 1, 2, 3]], [1, 0, [4, 5]], [1, 1, [0, 1, 2, 3]], [1, 1, [4, 5]], [2, 0, [0, 1, 2]], [2, 0, [3, 4]], [2, 1, [0, 1, 2]], [2, 1, [3, 4]], [3, 0, [0, 1, 2, 3]], [3, 1, [0, 1, 2, 3]], [4, 0, [0, 1, 2]], [4, 1, [0, 1]], [4, 1, [2]]]
 
         XV = [(3, 0, 0), (3, 1, 0), (4, 0, 0)]
-        HEAD = [['x', 0, 1, False, []], ['w', 0, 1, True, []], ['w', 0, 2, True, []], ['x', 1, 2, True, []], ['x', 2, 4, True, []]]
-        GROUPS = {0: [['x', 4, 7, False, [2]]], 1: [['w', 1, 0, True, [3]]], 2: [['w', 2, 0, False, [3]]], 3: [['w', 3, 0, True, [3]]], 4: [['c', 0, 4, True, [1, 3]], ['c', 4, 7, True, [0, 2]]], 5: [['w', 4, 0, False, [3]]], 6: [['w', 5, 0, True, [3]]], 7: [['w', 6, 0, False, [3]]], 8: [['w', 7, 0, True, [3]]], 9: [['w', 8, 0, False, [3]]], 10: [['w', 9, 0, True, [3]]]}
-        JOBS = {6: [['scores', 0, 4], ['max', 0, 4]], 7: [['exp', 0, 4], ['diag', 0, 4]], 8: [['scores', 4, 8], ['max', 4, 8]], 9: [['exp', 4, 8], ['diag', 4, 8]], 10: [['scores', 8, 12], ['max', 8, 12]], 11: [['exp', 8, 12], ['diag', 8, 12]], 12: [['scores', 12, 16], ['max', 12, 16]], 13: [['exp', 12, 16], ['diag', 12, 16]], 14: [['scores', 16, 18], ['max', 16, 18]], 15: [['exp', 16, 18], ['diag', 16, 18], ['scores', 18, 22], ['max', 18, 22]]}
+        HEAD = [['x', 0, 1, False, []], ['w', 0, 1, False, []], ['w', 0, 2, False, []], ['x', 1, 2, False, []], ['x', 2, 4, False, []]]
+        GROUPS = {0: [['x', 4, 7, False, []]], 1: [['w', 1, 0, True, [3]]], 2: [['w', 2, 0, True, [3]]], 3: [['w', 3, 0, True, [3]]], 4: [['c', 0, 4, True, []], ['c', 4, 7, True, []]], 5: [['w', 4, 0, True, [3]]], 6: [['w', 5, 0, True, [3]]], 7: [['w', 6, 0, True, [3]]], 8: [['w', 7, 0, True, [3]]], 9: [['w', 8, 0, True, [3]]], 10: [['w', 9, 0, True, [3]]]}
+        JOBS = {7: [['scores', 0, 4], ['max', 0, 4]], 8: [['exp', 0, 4], ['diag', 0, 4]], 9: [['scores', 4, 8], ['max', 4, 8]], 10: [['exp', 4, 8], ['diag', 4, 8]], 11: [['scores', 8, 12], ['max', 8, 12]], 12: [['exp', 8, 12], ['diag', 8, 12], ['scores', 12, 16], ['max', 12, 16]], 13: [['exp', 12, 16], ['diag', 12, 16]], 14: [['scores', 16, 18], ['max', 16, 18]], 15: [['exp', 16, 18], ['diag', 16, 18], ['scores', 18, 22], ['max', 18, 22]]}
         SPLIT_AT = 18
         ready = {}
         def prepare(grp_spec):
@@ -319,9 +319,10 @@ def tile_infonceloss_pa_kernel(tc, embeddings, contexts, W, out):
                     n_prep += 1
                 staged.append(turn(g))
                 n_turn += 1
-            while n_prep < min(n_turn + 2, len(flatg)) and GROUPS.get(j, []):
-                prepare(flatg[n_prep])
-                n_prep += 1
+            if j >= 1:
+                while n_prep < min(n_turn + 2, len(flatg)) and GROUPS.get(j, []):
+                    prepare(flatg[n_prep])
+                    n_prep += 1
             for job in JOBS.get(j, []):
                 if job[0] == "scores":
                     scores(job[1], job[2])
@@ -337,6 +338,9 @@ def tile_infonceloss_pa_kernel(tc, embeddings, contexts, W, out):
             waiting = []
             for w in staged:
                 quantise_tiles(*w)
+            while n_prep < min(n_turn + 2, len(flatg)) and GROUPS.get(j, []):
+                prepare(flatg[n_prep])
+                n_prep += 1
             k, g2, slices = chunks[j]
             unquantised.append((k, g2, slices, stage1(k, g2, slices)))
             for job in JOBS.get(j, []):
@@ -373,7 +377,7 @@ def tile_infonceloss_pa_kernel(tc, embeddings, contexts, W, out):
         for u in unquantised:
             quantise_xw(*u)
         scores(24, 25)
-
+        diagonal(18, 20)
         row_max(24, 25)
         exponentials(22, 24)
         exponentials(24, 25)
@@ -385,7 +389,7 @@ def tile_infonceloss_pa_kernel(tc, embeddings, contexts, W, out):
         zd0 = folded(early_d, B_LO * SPLIT_AT, "zd0")
         late_s = spread_sum(SPLIT_AT, N_GROUP, "spread_s1")
         zs1 = folded(late_s, B_LO * (N_GROUP - SPLIT_AT), "zs1")
-        diagonal(18, 22); diagonal(22, 25)
+        diagonal(20, 25)
         late_d = spread_diagonal(SPLIT_AT, N_GROUP, "spread_d1")
         zd1 = folded(late_d, B_LO * (N_GROUP - SPLIT_AT), "zd1")
         loss(zs0, zd0, 0, SPLIT_AT, range(3))

@@ -119,26 +119,22 @@ def tile_infonceloss_pa_kernel(tc, embeddings, contexts, W, out):
                     quantise(codes[:, i0 : i0 + w, :], scales[:, i0 : i0 + w, :], grp[:, i0 : i0 + w, :])
                     i0 += w
 
-        def split_words(raw_tiles, n):
+        def split_words(raw_tiles, n, run):
             split = split_pool.tile([P, 4, FEAT], BF16, name="split", tag="split")
             nc.vector.tensor_copy(
-                out=flat(split[:, 0:n, :]).bitcast(F32).rearrange("p (a u r) -> p a u r", u=2, r=P),
-                in_=flat(raw_tiles).bitcast(F32).rearrange("p (a r u) -> p a u r", u=2, r=P),
+                out=flat(split[:, 0:n, :]).rearrange("p (u m i) -> p u m i", u=2, i=run),
+                in_=flat(raw_tiles).rearrange("p (m u i) -> p u m i", u=2, i=run),
             )
-            return split[:, 0:n, :]
+            return flat(split[:, 0:n, :]).bitcast(F32)
 
         def transposes(rows, n, is_split, on_vector):
             grp = grp_pool.tile([P, 4, FEAT], BF16, name="grp", tag="grp", align_bytes=64)
             for i in range(n):
                 bank = ring.tile([P, 4, P], F32, name="bank", tag="bank")
-                words = rows[:, i, :].bitcast(F32)
                 for j in range(4):
                     g, u = j // 2, j % 2
-                    if is_split:
-                        col = words[:, P * j : P * (j + 1)]
-                    else:
-                        col = words[:, 256 * g + u : 256 * (g + 1) : 2]
-                    nc.tensor.transpose(bank[:, j, :], col, ident[:])
+                    first = (2 * n * u + 2 * i + g) * P
+                    nc.tensor.transpose(bank[:, j, :], rows[:, first : first + P], ident[:])
                 dst = grp[:, i, :].bitcast(F32).rearrange("p (g r u) -> p g r u", g=2, u=2)
                 src = bank[:].rearrange("p (g u) r -> p g r u", u=2)
                 if i in on_vector:
@@ -272,15 +268,15 @@ def tile_infonceloss_pa_kernel(tc, embeddings, contexts, W, out):
         chunks = [[0, 0, [0, 1, 2, 3]], [0, 0, [4, 5, 6]], [0, 1, [0, 1, 2, 3]], [0, 1, [4, 5, 6]], [1, 0, [0, 1, 2, 3]], [1, 0, [4, 5]], [1, 1, [0, 1, 2, 3]], [1, 1, [4, 5]], [2, 0, [0, 1, 2]], [2, 0, [3, 4]], [2, 1, [0, 1, 2]], [2, 1, [3, 4]], [3, 0, [0, 1, 2, 3]], [3, 1, [0, 1, 2, 3]], [4, 0, [0, 1, 2]], [4, 1, [0, 1]], [4, 1, [2]]]
 
         XV = [(3, 0, 0), (3, 1, 0), (4, 0, 0)]
-        HEAD = [['x', 0, 1, False, []], ['w', 0, 1, False, []], ['w', 0, 2, False, []], ['x', 1, 2, False, []], ['x', 2, 4, False, []]]
-        GROUPS = {0: [['x', 4, 7, False, []]], 1: [['w', 1, 0, True, [3]]], 2: [['w', 2, 0, True, [3]]], 3: [['w', 3, 0, True, [3]]], 4: [['c', 0, 4, True, []], ['c', 4, 7, True, []]], 5: [['w', 4, 0, True, [3]]], 6: [['w', 5, 0, True, [3]]], 7: [['w', 6, 0, True, [3]]], 8: [['w', 7, 0, True, [3]]], 9: [['w', 8, 0, True, [3]]], 10: [['w', 9, 0, True, [3]]]}
+        HEAD = [['x', 0, 1, True, []], ['w', 0, 1, True, []], ['w', 0, 2, True, []], ['x', 1, 2, True, []], ['x', 2, 4, True, []]]
+        GROUPS = {0: [['x', 4, 7, True, []]], 1: [['w', 1, 0, True, [3]]], 2: [['w', 2, 0, True, [3]]], 3: [['w', 3, 0, True, [3]]], 4: [['c', 0, 4, True, []], ['c', 4, 7, True, []]], 5: [['w', 4, 0, True, [3]]], 6: [['w', 5, 0, True, [3]]], 7: [['w', 6, 0, True, [3]]], 8: [['w', 7, 0, True, [3]]], 9: [['w', 8, 0, True, [3]]], 10: [['w', 9, 0, True, [3]]]}
         JOBS = {7: [['scores', 0, 4], ['max', 0, 4]], 8: [['exp', 0, 4], ['diag', 0, 4]], 9: [['scores', 4, 8], ['max', 4, 8]], 10: [['exp', 4, 8], ['diag', 4, 8]], 11: [['scores', 8, 12], ['max', 8, 12]], 12: [['exp', 8, 12], ['diag', 8, 12], ['scores', 12, 16], ['max', 12, 16]], 13: [['exp', 12, 16], ['diag', 12, 16]], 14: [['scores', 16, 18], ['max', 16, 18]], 15: [['exp', 16, 18], ['diag', 16, 18], ['scores', 18, 22], ['max', 18, 22]]}
         SPLIT_AT = 18
         ready = {}
         def prepare(grp_spec):
             kind, a, b, is_split, on_v = grp_spec
             raw_tiles, n, codes, scales = operand(kind, a, b)
-            ready[kind, a, b] = split_words(raw_tiles, n) if is_split else raw_tiles
+            ready[kind, a, b] = split_words(raw_tiles, n, 2 if kind == "c" else 16)
             if is_split:
                 reload(grp_spec)
 

@@ -133,8 +133,12 @@ def tile_infonceloss_pa_kernel(tc, embeddings, contexts, W, out):
                 bank = ring.tile([P, 4, P], F32, name="bank", tag="bank")
                 for j in range(4):
                     g, u = j // 2, j % 2
-                    first = (2 * n * u + 2 * i + g) * P
-                    nc.tensor.transpose(bank[:, j, :], rows[:, first : first + P], ident[:])
+                    if is_split:
+                        first = (2 * n * u + 2 * i + g) * P
+                        col = rows[:, first : first + P]
+                    else:
+                        col = rows[:, i, :].bitcast(F32)[:, 256 * g + u : 256 * (g + 1) : 2]
+                    nc.tensor.transpose(bank[:, j, :], col, ident[:])
                 dst = grp[:, i, :].bitcast(F32).rearrange("p (g r u) -> p g r u", g=2, u=2)
                 src = bank[:].rearrange("p (g u) r -> p g r u", u=2)
                 if i in on_vector:
@@ -269,14 +273,14 @@ def tile_infonceloss_pa_kernel(tc, embeddings, contexts, W, out):
 
         XV = [(3, 0, 0), (3, 1, 0), (4, 0, 0)]
         HEAD = [['x', 0, 1, True, []], ['w', 0, 1, True, []], ['w', 0, 2, True, []], ['x', 1, 2, True, []], ['x', 2, 4, True, []]]
-        GROUPS = {0: [['x', 4, 7, True, []]], 1: [['w', 1, 0, True, [3]]], 2: [['w', 2, 0, True, [3]]], 3: [['w', 3, 0, True, [3]]], 4: [['c', 0, 4, True, []], ['c', 4, 7, True, []]], 5: [['w', 4, 0, True, [3]]], 6: [['w', 5, 0, True, [3]]], 7: [['w', 6, 0, True, [3]]], 8: [['w', 7, 0, True, [3]]], 9: [['w', 8, 0, True, [3]]], 10: [['w', 9, 0, True, [3]]]}
+        GROUPS = {0: [['x', 4, 7, True, []]], 1: [['w', 1, 0, True, [3]]], 2: [['w', 2, 0, True, [3]]], 3: [['w', 3, 0, True, [3]]], 4: [['c', 0, 4, True, [3]], ['c', 4, 7, True, [2]]], 5: [['w', 4, 0, True, [3]]], 6: [['w', 5, 0, True, [3]]], 7: [['w', 6, 0, True, [3]]], 8: [['w', 7, 0, True, [3]]], 9: [['w', 8, 0, True, [3]]], 10: [['w', 9, 0, True, [3]]]}
         JOBS = {7: [['scores', 0, 4], ['max', 0, 4]], 8: [['exp', 0, 4], ['diag', 0, 4]], 9: [['scores', 4, 8], ['max', 4, 8]], 10: [['exp', 4, 8], ['diag', 4, 8]], 11: [['scores', 8, 12], ['max', 8, 12]], 12: [['exp', 8, 12], ['diag', 8, 12], ['scores', 12, 16], ['max', 12, 16]], 13: [['exp', 12, 16], ['diag', 12, 16]], 14: [['scores', 16, 18], ['max', 16, 18]], 15: [['exp', 16, 18], ['diag', 16, 18], ['scores', 18, 22], ['max', 18, 22]]}
         SPLIT_AT = 18
         ready = {}
         def prepare(grp_spec):
             kind, a, b, is_split, on_v = grp_spec
             raw_tiles, n, codes, scales = operand(kind, a, b)
-            ready[kind, a, b] = split_words(raw_tiles, n, 2 if kind == "c" else 16)
+            ready[kind, a, b] = split_words(raw_tiles, n, 2 if kind == "c" else 16) if is_split else raw_tiles
             if is_split:
                 reload(grp_spec)
 
@@ -293,18 +297,26 @@ def tile_infonceloss_pa_kernel(tc, embeddings, contexts, W, out):
                 reload(grp_spec)
             return grp, n, codes, scales
 
+        order = sorted(GROUPS)
+        flatg = [g for j in order for g in GROUPS[j]]
+        if True:
+            masks()
         waiting = []
-        prepare(HEAD[0])
+        ahead = HEAD + flatg[0:1]
+        n_head = 0
         for i in range(len(HEAD)):
-            if i + 1 < len(HEAD):
-                prepare(HEAD[i + 1])
+            while n_head < min(i + 1 + 2, len(ahead)):
+                prepare(ahead[n_head])
+                n_head += 1
             waiting.append(turn(HEAD[i]))
             if i >= 1:
                 quantise_tiles(*waiting.pop(0))
-        masks()
-        order = sorted(GROUPS)
-        flatg = [g for j in order for g in GROUPS[j]]
-        n_prep = 0
+        while n_head < len(ahead):
+            prepare(ahead[n_head])
+            n_head += 1
+        if not True:
+            masks()
+        n_prep = 1
         n_turn = 0
         unquantised = []
         for j in range(len(chunks)):
@@ -361,7 +373,7 @@ def tile_infonceloss_pa_kernel(tc, embeddings, contexts, W, out):
         def store(k):
             n_s = N_SLICE - k
             g0 = GROUP0[k]
-            queue = nc.sync if k % 2 == 0 else nc.scalar
+            queue = nc.scalar if k == 3 else nc.sync
             queue.dma_start(
                 out=out[P * g0 : P * (g0 + n_s)].rearrange("(q c) -> q c", q=B_HI),
                 in_=res[k][0:B_HI, :, :].rearrange("q l s -> q (l s)"),
@@ -369,16 +381,16 @@ def tile_infonceloss_pa_kernel(tc, embeddings, contexts, W, out):
 
         exponentials(18, 22)
         scores(22, 24)
-        row_max(22, 24)
         for u in unquantised:
             quantise_xw(*u)
         scores(24, 25)
-        diagonal(18, 20)
+        row_max(22, 24)
+
         row_max(24, 25)
         exponentials(22, 24)
         exponentials(24, 25)
         nc.scalar.activation(out=warm[:, 1:2], in_=sumexp[:, N_GROUP - 1 : N_GROUP], func=ACT.Ln)
-
+        diagonal(18, 20)
         early_s = spread_sum(0, SPLIT_AT, "spread_s0")
         early_d = spread_diagonal(0, SPLIT_AT, "spread_d0")
         zs0 = folded(early_s, B_LO * SPLIT_AT, "zs0")

@@ -269,12 +269,12 @@ def tile_infonceloss_pa_kernel(tc, embeddings, contexts, W, out):
             nc.tensor.matmul(tile[:, 0:n], lhsT=fold[:], rhs=src, start=True, stop=True)
             return tile
 
-        chunks = [[0, 0, [0, 1, 2, 3]], [0, 0, [4, 5, 6]], [0, 1, [0, 1, 2, 3]], [0, 1, [4, 5, 6]], [1, 0, [0, 1, 2, 3]], [1, 0, [4, 5]], [1, 1, [0, 1, 2, 3]], [1, 1, [4, 5]], [2, 0, [0, 1, 2]], [2, 0, [3, 4]], [2, 1, [0, 1, 2]], [2, 1, [3, 4]], [3, 0, [0, 1, 2, 3]], [3, 1, [0, 1, 2, 3]], [4, 0, [0, 1, 2]], [4, 1, [0, 1]], [4, 1, [2]]]
+        chunks = [[0, 0, [0, 1]], [0, 0, [2, 3]], [0, 0, [4, 5, 6]], [0, 1, [0, 1, 2, 3]], [0, 1, [4, 5, 6]], [1, 0, [0, 1, 2, 3]], [1, 0, [4, 5]], [1, 1, [0, 1, 2, 3]], [1, 1, [4, 5]], [2, 0, [0, 1, 2]], [2, 0, [3, 4]], [2, 1, [0, 1, 2]], [2, 1, [3, 4]], [3, 0, [0, 1, 2, 3]], [3, 1, [0, 1, 2, 3]], [4, 0, [0, 1, 2]], [4, 1, [0, 1]], [4, 1, [2]]]
 
         XV = [(3, 0, 0), (3, 1, 0), (4, 0, 0)]
-        HEAD = [['x', 0, 1, True, []], ['w', 0, 1, True, []], ['w', 0, 2, True, []], ['x', 1, 2, True, []], ['x', 2, 4, True, []]]
-        GROUPS = {0: [['x', 4, 7, True, []]], 1: [['w', 1, 0, True, [3]]], 2: [['w', 2, 0, True, [3]]], 3: [['w', 3, 0, True, [3]]], 4: [['c', 0, 4, True, [3]], ['c', 4, 7, True, [2]]], 5: [['w', 4, 0, True, [3]]], 6: [['w', 5, 0, True, [3]]], 7: [['w', 6, 0, True, [3]]], 8: [['w', 7, 0, True, [3]]], 9: [['w', 8, 0, True, [3]]], 10: [['w', 9, 0, True, [3]]]}
-        JOBS = {7: [['scores', 0, 4], ['max', 0, 4]], 8: [['exp', 0, 4], ['diag', 0, 4]], 9: [['scores', 4, 8], ['max', 4, 8]], 10: [['exp', 4, 8], ['diag', 4, 8]], 11: [['scores', 8, 12], ['max', 8, 12]], 12: [['exp', 8, 12], ['diag', 8, 12], ['scores', 12, 16], ['max', 12, 16]], 13: [['exp', 12, 16], ['diag', 12, 16]], 14: [['scores', 16, 18], ['max', 16, 18]], 15: [['exp', 16, 18], ['diag', 16, 18], ['scores', 18, 22], ['max', 18, 22]]}
+        HEAD = [['x', 0, 1, True, []], ['w', 0, 1, True, []], ['w', 0, 2, True, []], ['x', 1, 2, True, []]]
+        GROUPS = {0: [['x', 2, 4, True, []]], 1: [['x', 4, 7, True, []]], 2: [['w', 1, 0, True, [3]]], 3: [['w', 2, 0, True, [3]]], 4: [['w', 3, 0, True, [3]]], 5: [['c', 0, 4, True, [3]], ['c', 4, 7, True, [2]]], 6: [['w', 4, 0, True, [3]]], 7: [['w', 5, 0, True, [3]]], 8: [['w', 6, 0, True, [3]]], 9: [['w', 7, 0, True, [3]]], 10: [['w', 8, 0, True, [3]]], 11: [['w', 9, 0, True, [3]]]}
+        JOBS = {8: [['scores', 0, 4], ['max', 0, 4]], 9: [['exp', 0, 4], ['diag', 0, 4]], 10: [['scores', 4, 8], ['max', 4, 8]], 11: [['exp', 4, 8], ['diag', 4, 8]], 12: [['scores', 8, 12], ['max', 8, 12]], 13: [['exp', 8, 12], ['diag', 8, 12], ['scores', 12, 16], ['max', 12, 16]], 14: [['exp', 12, 16], ['diag', 12, 16]], 15: [['scores', 16, 18], ['max', 16, 18]], 16: [['exp', 16, 18], ['diag', 16, 18], ['scores', 18, 22], ['max', 18, 22], ['diag', 18, 20]]}
         SPLIT_AT = 18
         ready = {}
         def prepare(grp_spec):
@@ -327,6 +327,12 @@ def tile_infonceloss_pa_kernel(tc, embeddings, contexts, W, out):
                     n_prep += 1
                 staged.append(turn(g))
                 n_turn += 1
+            if j == 0:
+                for w in waiting:
+                    quantise_tiles(*w)
+                waiting = []
+                prepare(flatg[n_prep])
+                n_prep += 1
             if j >= 1:
                 while n_prep < min(n_turn + 2, len(flatg)) and GROUPS.get(j, []):
                     prepare(flatg[n_prep])
@@ -390,7 +396,7 @@ def tile_infonceloss_pa_kernel(tc, embeddings, contexts, W, out):
         exponentials(22, 24)
         exponentials(24, 25)
         nc.scalar.activation(out=warm[:, 1:2], in_=sumexp[:, N_GROUP - 1 : N_GROUP], func=ACT.Ln)
-        diagonal(18, 20)
+
         early_s = spread_sum(0, SPLIT_AT, "spread_s0")
         early_d = spread_diagonal(0, SPLIT_AT, "spread_d0")
         zs0 = folded(early_s, B_LO * SPLIT_AT, "zs0")

from contextlib import ExitStack

import concourse.mybir as mybir
from concourse.masks import make_identity

F32 = mybir.dt.float32
BF16 = mybir.dt.bfloat16
U32 = mybir.dt.uint32
U8 = mybir.dt.uint8
FP8X4 = mybir.dt.float8_e4m3fn_x4
ALU = mybir.AluOpType
ACT = mybir.ActivationFunctionType
AX = mybir.AxisListType

P = 128
FEAT = 1024
N_STEP = 5
N_SLICE = 7
TILE_WORDS = FEAT // 4
GROUP0 = [0, 7, 13, 18, 22]
N_GROUP = 25
B_LO = 8
B_HI = P // B_LO
W_BUFFERS = 5
FLOPS = 2 * N_GROUP * P * FEAT * FEAT + 2 * N_GROUP * P * P * FEAT


def tile_infonceloss_pa_kernel(tc, embeddings, contexts, W, out):
    nc = tc.nc
    with ExitStack() as ctx:
        const = ctx.enter_context(tc.tile_pool(name="const", bufs=1))
        raw = ctx.enter_context(tc.tile_pool(name="raw", bufs=1))
        wraw_pool = ctx.enter_context(tc.tile_pool(name="wraw", bufs=W_BUFFERS))
        split_pool = ctx.enter_context(tc.tile_pool(name="split", bufs=3))
        grp_pool = ctx.enter_context(tc.tile_pool(name="grp", bufs=4))
        keep = ctx.enter_context(tc.tile_pool(name="keep", bufs=1))
        xwg_pool = ctx.enter_context(tc.tile_pool(name="xwg", bufs=2))
        junk = ctx.enter_context(tc.tile_pool(name="junk", bufs=2))
        ring = ctx.enter_context(tc.psum_pool(name="ring", bufs=6))
        scp = ctx.enter_context(tc.psum_pool(name="scores", bufs=8 - 6))
        ctx.enter_context(tc.manual_schedule())

        x_raw = raw.tile([P, N_SLICE, FEAT], BF16, name="x_raw")
        c_raw = raw.tile([P, N_SLICE, FEAT], BF16, name="c_raw")
        w_raw = {}

        def load_x(t0, t1):
            nc.sync.dma_start(out=x_raw[:, t0:t1, :], in_=embeddings[:, 1 + t0 : 1 + t1, :])

        def load_c(t0, t1):
            nc.sync.dma_start(out=c_raw[:, t0:t1, :], in_=contexts[:, t0:t1, :])

        def load_w(half, pieces=1):
            k, g = half // 2, half % 2
            w_half = wraw_pool.tile([P, 4, FEAT], BF16, name="w_raw", tag="w_raw")
            src = W[k, 512 * g : 512 * (g + 1), :].rearrange("(p t) d -> p t d", t=4)
            step = 4 // pieces
            for t in range(0, 4, step):
                nc.sync.dma_start(out=w_half[:, t : t + step, :], in_=src[:, t : t + step, :])
            w_raw[half] = w_half

        for kind, a, b in [['x', 0, 1], ['w', 0, 2], ['x', 1, 2], ['x', 2, 4], ['x', 4, 7], ['w', 1, 1], ['w', 2, 1], ['w', 3, 1], ['c', 0, 4], ['c', 4, 7], ['w', 4, 1]]:
            if kind == "x":
                load_x(a, b)
            elif kind == "c":
                load_c(a, b)
            else:
                load_w(a, b)

        ident = const.tile([P, P], F32, name="ident")
        make_identity(nc, ident[:])
        warm = const.tile([P, 2], F32, name="warm")
        nc.vector.memset(warm[:], 1.0)
        nc.scalar.activation(out=warm[:, 1:2], in_=warm[:, 0:1], func=ACT.Exp)
        mask8 = const.tile([P, B_LO], F32, name="mask8")
        fold = const.tile([P, P], F32, name="fold")
        mask_s = const.tile([P, B_LO, N_GROUP], F32, name="mask_s")

        def masks():
            nc.vector.tensor_reduce(
                out=mask8[:], in_=ident[:].rearrange("p (q l) -> p l q", l=B_LO), axis=AX.X, op=ALU.add
            )
            nc.vector.memset(fold[:], 0.0)
            nc.vector.tensor_reduce(
                out=fold[:, 0:B_HI], in_=ident[:].rearrange("p (q l) -> p q l", l=B_LO), axis=AX.X, op=ALU.add
            )
            for k in range(N_STEP):
                n_s = N_SLICE - k
                nc.vector.tensor_scalar(
                    out=mask_s[:, :, GROUP0[k] : GROUP0[k] + n_s],
                    in0=mask8[:].unsqueeze(2).to_broadcast([P, B_LO, n_s]),
                    scalar1=1.0 / (P * n_s),
                    scalar2=None,
                    op0=ALU.mult,
                )

        xq = keep.tile([P, N_SLICE, TILE_WORDS], U32, name="xq", align_bytes=64)
        xs = keep.tile([P, N_SLICE, TILE_WORDS], U8, name="xs", align_bytes=64)
        cq = keep.tile([P, N_SLICE, TILE_WORDS], U32, name="cq", align_bytes=64)
        cs = keep.tile([P, N_SLICE, TILE_WORDS], U8, name="cs", align_bytes=64)
        wq = [keep.tile([P, 8, TILE_WORDS], U32, name="wq%d" % k, align_bytes=64) for k in range(N_STEP)]
        ws = [keep.tile([P, 8, TILE_WORDS], U8, name="ws%d" % k, align_bytes=64) for k in range(N_STEP)]
        xwq = keep.tile([P, 2 * N_GROUP, P], U32, name="xwq", align_bytes=64)
        xws = keep.tile([P, 2 * N_GROUP, P], U8, name="xws", align_bytes=64)
        negmax = keep.tile([P, N_GROUP], F32, name="negmax")
        sumexp = keep.tile([P, N_GROUP], F32, name="sumexp")
        dm = keep.tile([P, N_GROUP], F32, name="dm")

        def flat(ap):
            return ap.rearrange("p i c -> p (i c)")

        def quantise(codes, scales, values):
            nc.vector.quantize_mx(out=flat(codes).bitcast(FP8X4), scales=flat(scales), in_=flat(values))

        def quantise_tiles(grp, n, codes, scales):
            i0 = 0
            for w in (4, 2, 1):
                for call in range((n - i0) // w):
                    quantise(codes[:, i0 : i0 + w, :], scales[:, i0 : i0 + w, :], grp[:, i0 : i0 + w, :])
                    i0 += w

        def split_words(raw_tiles, n, run):
            split = split_pool.tile([P, 4, FEAT], BF16, name="split", tag="split")
            nc.vector.tensor_copy(
                out=flat(split[:, 0:n, :]).rearrange("p (u m i) -> p u m i", u=2, i=run),
                in_=flat(raw_tiles).rearrange("p (m u i) -> p u m i", u=2, i=run),
            )
            return flat(split[:, 0:n, :]).bitcast(F32)

        def transposes(rows, n, is_split, on_vector):
            grp = grp_pool.tile([P, 4, FEAT], BF16, name="grp", tag="grp", align_bytes=64)
            for i in range(n):
                bank = ring.tile([P, 4, P], F32, name="bank", tag="bank")
                for j in range(4):
                    g, u = j // 2, j % 2
                    if is_split:
                        first = (2 * n * u + 2 * i + g) * P
                        col = rows[:, first : first + P]
                    else:
                        col = rows[:, i, :].bitcast(F32)[:, 256 * g + u : 256 * (g + 1) : 2]
                    nc.tensor.transpose(bank[:, j, :], col, ident[:])
                dst = grp[:, i, :].bitcast(F32).rearrange("p (g r u) -> p g r u", g=2, u=2)
                src = bank[:].rearrange("p (g u) r -> p g r u", u=2)
                if i in on_vector:
                    nc.vector.tensor_copy(out=dst, in_=src)
                else:
                    nc.scalar.copy(out=dst, in_=src)
            return grp

        def operand(kind, a, b):
            if kind == "x":
                return x_raw[:, a:b, :], b - a, xq[:, a:b, :], xs[:, a:b, :]
            if kind == "c":
                return c_raw[:, a:b, :], b - a, cq[:, a:b, :], cs[:, a:b, :]
            k, g = a // 2, a % 2
            t0, t1 = {0: (0, 4), 1: (0, 2), 2: (2, 4)}[b]
            tiles = slice(4 * g + t0, 4 * g + t1)
            return w_raw[a][:, t0:t1, :], t1 - t0, wq[k][:, tiles, :], ws[k][:, tiles, :]

        def xw_row(k, g2, s):
            return 2 * GROUP0[k] + g2 * (N_SLICE - k) + s

        def stage1(k, g2, slices):
            xwg = xwg_pool.tile([P, 4, 512], BF16, name="xwg", tag="xwg", align_bytes=64)
            for i in range(len(slices)):
                s = slices[i]
                bank = ring.tile([P, 4, P], F32, name="bank", tag="bank")
                for t in range(4):
                    for g1 in range(2):
                        cols = slice(P * g1, P * (g1 + 1))
                        nc.tensor.matmul_mx(
                            out=bank[:, t, :],
                            lhsT=wq[k][:, 4 * g2 + t, cols].bitcast(FP8X4),
                            lhsT_scale=ws[k][:, 4 * g2 + t, cols],
                            rhs=xq[:, k + s, cols].bitcast(FP8X4),
                            rhs_scale=xs[:, k + s, cols],
                            start=(g1 == 0),
                            stop=(g1 == 1),
                        )
                copy = nc.vector.tensor_copy if (k, g2, s) in XV else nc.scalar.copy
                copy(
                    out=xwg[:, i, :].rearrange("p (b t) -> p b t", t=4),
                    in_=bank[:].rearrange("p t b -> p b t"),
                )
            return xwg

        def quantise_xw(k, g2, slices, xwg):
            n = len(slices)
            r0 = xw_row(k, g2, slices[0])
            i0 = 0
            for w in (4, 2, 1):
                for call in range((n - i0) // w):
                    quantise(xwq[:, r0 + i0 : r0 + i0 + w, :], xws[:, r0 + i0 : r0 + i0 + w, :], xwg[:, i0 : i0 + w, :])
                    i0 += w

        pairs = [(k, s) for k in range(N_STEP) for s in range(N_SLICE - k)]
        score_bank = {}

        def scores(p0, p1):
            if p0 == 24:
                sc = ring.tile([P, 4, P], F32, name="sc_last", tag="bank")
            else:
                sc = scp.tile([P, 4, P], F32, name="sc", tag="sc")
            for i in range(p1 - p0):
                k, s = pairs[p0 + i]
                for g2 in range(2):
                    r = xw_row(k, g2, s)
                    cols = slice(P * g2, P * (g2 + 1))
                    nc.tensor.matmul_mx(
                        out=sc[:, i, :],
                        lhsT=xwq[:, r, :].bitcast(FP8X4),
                        lhsT_scale=xws[:, r, :],
                        rhs=cq[:, s, cols].bitcast(FP8X4),
                        rhs_scale=cs[:, s, cols],
                        start=(g2 == 0),
                        stop=(g2 == 1),
                    )
                score_bank[p0 + i] = sc[:, i, :]
            score_bank["bank", p0] = sc

        def row_max(p0, p1):
            sc = score_bank["bank", p0]
            nc.vector.tensor_reduce(out=negmax[:, p0:p1], in_=sc[:, 0 : p1 - p0, :], axis=AX.X, op=ALU.max, negate=True)

        def diagonal(p0, p1):
            for p in range(p0, p1):
                jv = junk.tile([P, P], F32, name="jv", tag="jv")
                nc.vector.scalar_tensor_tensor(
                    out=jv[:],
                    in0=score_bank[p],
                    scalar=negmax[:, p : p + 1],
                    in1=ident[:],
                    op0=ALU.add,
                    op1=ALU.mult,
                    accum_out=dm[:, p : p + 1],
                )

        def exponentials(p0, p1):
            for p in range(p0, p1):
                js = junk.tile([P, P], F32, name="js", tag="js")
                nc.scalar.activation(
                    out=js[:],
                    in_=score_bank[p],
                    func=ACT.Exp,
                    bias=negmax[:, p : p + 1],
                    scale=1.0,
                    accum_out=sumexp[:, p : p + 1],
                )

        def spread(p0, p1, values, mask, name):
            n = p1 - p0
            tile = keep.tile([P, B_LO, n], F32, name=name)
            nc.vector.tensor_tensor(
                out=tile[:],
                in0=values[:, p0:p1].unsqueeze(1).to_broadcast([P, B_LO, n]),
                in1=mask,
                op=ALU.mult,
            )
            return tile[:].rearrange("p l s -> p (l s)")

        def spread_sum(p0, p1, name):
            return spread(p0, p1, sumexp, mask_s[:, :, p0:p1], name)

        def spread_diagonal(p0, p1, name):
            return spread(p0, p1, dm, mask8[:].unsqueeze(2).to_broadcast([P, B_LO, p1 - p0]), name)

        def folded(src, n, name):
            tile = ring.tile([P, 512], F32, name=name, tag="bank")
            nc.tensor.matmul(tile[:, 0:n], lhsT=fold[:], rhs=src, start=True, stop=True)
            return tile

        chunks = [[0, 0, [0, 1]], [0, 0, [2, 3]], [0, 0, [4, 5, 6]], [0, 1, [0, 1, 2, 3]], [0, 1, [4, 5, 6]], [1, 0, [0, 1, 2, 3]], [1, 0, [4, 5]], [1, 1, [0, 1, 2, 3]], [1, 1, [4, 5]], [2, 0, [0, 1, 2]], [2, 0, [3, 4]], [2, 1, [0, 1, 2]], [2, 1, [3, 4]], [3, 0, [0, 1, 2, 3]], [3, 1, [0, 1, 2, 3]], [4, 0, [0, 1, 2]], [4, 1, [0, 1]], [4, 1, [2]]]

        XV = [(3, 0, 0), (3, 1, 0), (4, 0, 0)]
        HEAD = [['x', 0, 1, True, []], ['w', 0, 1, True, []], ['w', 0, 2, True, []], ['x', 1, 2, True, []]]
        GROUPS = {0: [['x', 2, 4, True, []]], 1: [['x', 4, 7, True, []]], 2: [['w', 1, 0, True, [3]]], 3: [['w', 2, 0, True, [3]]], 4: [['w', 3, 0, True, [3]]], 5: [['c', 0, 4, True, [3]], ['c', 4, 7, True, [2]]], 6: [['w', 4, 0, True, [3]]], 7: [['w', 5, 0, True, [3]]], 8: [['w', 6, 0, True, [3]]], 9: [['w', 7, 0, True, [3]]], 10: [['w', 8, 0, True, [3]]], 11: [['w', 9, 0, True, [3]]]}
        JOBS = {8: [['scores', 0, 4], ['max', 0, 4]], 9: [['exp', 0, 4], ['diag', 0, 4]], 10: [['scores', 4, 8], ['max', 4, 8]], 11: [['exp', 4, 8], ['diag', 4, 8]], 12: [['scores', 8, 12], ['max', 8, 12]], 13: [['exp', 8, 12], ['diag', 8, 12], ['scores', 12, 16], ['max', 12, 16]], 14: [['exp', 12, 16], ['diag', 12, 16]], 15: [['scores', 16, 18], ['max', 16, 18]], 16: [['exp', 16, 18], ['diag', 16, 18], ['scores', 18, 22], ['max', 18, 22], ['diag', 18, 20]]}
        SPLIT_AT = 18
        ready = {}
        def prepare(grp_spec):
            kind, a, b, is_split, on_v = grp_spec
            raw_tiles, n, codes, scales = operand(kind, a, b)
            ready[kind, a, b] = split_words(raw_tiles, n, 2 if kind == "c" else 16) if is_split else raw_tiles
            if is_split:
                reload(grp_spec)

        def reload(grp_spec):
            kind, a, b = grp_spec[0:3]
            if kind == "w" and b != 1 and a + W_BUFFERS < 2 * N_STEP:
                load_w(a + W_BUFFERS)

        def turn(grp_spec):
            kind, a, b, is_split, on_v = grp_spec
            raw_tiles, n, codes, scales = operand(kind, a, b)
            grp = transposes(ready[kind, a, b], n, is_split, on_v)
            if not is_split:
                reload(grp_spec)
            return grp, n, codes, scales

        order = sorted(GROUPS)
        flatg = [g for j in order for g in GROUPS[j]]
        if True:
            masks()
        waiting = []
        ahead = HEAD + flatg[0:1]
        n_head = 0
        for i in range(len(HEAD)):
            while n_head < min(i + 1 + 2, len(ahead)):
                prepare(ahead[n_head])
                n_head += 1
            waiting.append(turn(HEAD[i]))
            if i >= 1:
                quantise_tiles(*waiting.pop(0))
        while n_head < len(ahead):
            prepare(ahead[n_head])
            n_head += 1
        if not True:
            masks()
        n_prep = 1
        n_turn = 0
        unquantised = []
        for j in range(len(chunks)):
            staged = []
            for g in GROUPS.get(j, []):
                while n_prep < min(n_turn + 1, len(flatg)):
                    prepare(flatg[n_prep])
                    n_prep += 1
                staged.append(turn(g))
                n_turn += 1
            if j == 0:
                for w in waiting:
                    quantise_tiles(*w)
                waiting = []
                prepare(flatg[n_prep])
                n_prep += 1
            if j >= 1:
                while n_prep < min(n_turn + 2, len(flatg)) and GROUPS.get(j, []):
                    prepare(flatg[n_prep])
                    n_prep += 1
            for job in JOBS.get(j, []):
                if job[0] == "scores":
                    scores(job[1], job[2])
                if job[0] == "exp":
                    exponentials(job[1], job[2])
            for job in JOBS.get(j, []):
                if job[0] == "max0":
                    row_max(job[1], job[2])
            while len(unquantised) > 0:
                quantise_xw(*unquantised.pop(0))
            for w in waiting:
                quantise_tiles(*w)
            waiting = []
            for w in staged:
                quantise_tiles(*w)
            while n_prep < min(n_turn + 2, len(flatg)) and GROUPS.get(j, []):
                prepare(flatg[n_prep])
                n_prep += 1
            k, g2, slices = chunks[j]
            unquantised.append((k, g2, slices, stage1(k, g2, slices)))
            for job in JOBS.get(j, []):
                if job[0] == "max":
                    row_max(job[1], job[2])
                if job[0] == "diag":
                    diagonal(job[1], job[2])
        lnz = keep.tile([P, B_LO * N_GROUP], F32, name="lnz")
        res = [keep.tile([P, B_LO, N_SLICE - k], F32, name="res%d" % k) for k in range(N_STEP)]

        def loss(zs, zd, p0, p1, steps):
            n = p1 - p0
            ln = lnz[0:B_HI, B_LO * p0 : B_LO * p1]
            nc.scalar.activation(out=ln, in_=zs[0:B_HI, 0 : B_LO * n], func=ACT.Ln)
            ln = ln.rearrange("q (l s) -> q l s", l=B_LO)
            dg = zd[0:B_HI, 0 : B_LO * n].rearrange("q (l s) -> q l s", l=B_LO)
            for k in steps:
                s0 = GROUP0[k] - p0
                s1 = s0 + N_SLICE - k
                nc.vector.tensor_tensor(out=res[k][0:B_HI, :, :], in0=ln[:, :, s0:s1], in1=dg[:, :, s0:s1], op=ALU.subtract)

        def store(k):
            n_s = N_SLICE - k
            g0 = GROUP0[k]
            queue = nc.scalar if k == 3 else nc.sync
            queue.dma_start(
                out=out[P * g0 : P * (g0 + n_s)].rearrange("(q c) -> q c", q=B_HI),
                in_=res[k][0:B_HI, :, :].rearrange("q l s -> q (l s)"),
            )

        exponentials(18, 22)
        scores(22, 24)
        for u in unquantised:
            quantise_xw(*u)
        scores(24, 25)
        row_max(22, 24)

        row_max(24, 25)
        exponentials(22, 24)
        exponentials(24, 25)
        nc.scalar.activation(out=warm[:, 1:2], in_=sumexp[:, N_GROUP - 1 : N_GROUP], func=ACT.Ln)

        early_s = spread_sum(0, SPLIT_AT, "spread_s0")
        early_d = spread_diagonal(0, SPLIT_AT, "spread_d0")
        zs0 = folded(early_s, B_LO * SPLIT_AT, "zs0")
        zd0 = folded(early_d, B_LO * SPLIT_AT, "zd0")
        late_s = spread_sum(SPLIT_AT, N_GROUP, "spread_s1")
        zs1 = folded(late_s, B_LO * (N_GROUP - SPLIT_AT), "zs1")
        diagonal(20, 25)
        late_d = spread_diagonal(SPLIT_AT, N_GROUP, "spread_d1")
        zd1 = folded(late_d, B_LO * (N_GROUP - SPLIT_AT), "zd1")
        loss(zs0, zd0, 0, SPLIT_AT, range(3))
        for k in range(3):
            store(k)
        loss(zs1, zd1, SPLIT_AT, N_GROUP, range(3, N_STEP))
        for k in range(3, N_STEP):
            store(k)
